import numpy as np
import ml_dtypes


def mxq(x, axis, fmt="e4m3"):
    dtype, down = {"e4m3": (ml_dtypes.float8_e4m3fn, 7), "e5m2": (ml_dtypes.float8_e5m2, 14)}[fmt]
    v = np.moveaxis(np.asarray(x, np.float32).astype(ml_dtypes.bfloat16).astype(np.float64), axis, -1)
    blocks = v.reshape(v.shape[:-1] + (-1, 32))
    amax = np.abs(blocks).max(-1, keepdims=True)
    byte = np.maximum(np.where(amax > 0, np.frexp(amax)[1] - 1 + 127, 0) - down, 1)
    scale = np.exp2(byte - 127.0)
    codes = (blocks / scale).astype(np.float32).astype(dtype).astype(np.float64)
    return np.moveaxis((codes * scale).reshape(v.shape), -1, axis)


WIDE = False


def mx_kscale(k):
    if not WIDE:
        return np.ones(k)
    levels = np.array([10, -10, 5, -5, 0])
    a = np.random.permutation(np.resize(levels, k // 512 * 4)).reshape(k // 512, 4)
    idx = np.arange(k)
    return np.exp2(a[idx // 512, idx % 128 // 32])


BF16 = ml_dtypes.bfloat16


def bf(x):
    return np.asarray(x, np.float32).astype(BF16)


def f64(x):
    return np.asarray(x).astype(np.float64)


B, C, D, R, STEPS = 256, 8192, 1024, 4, 5
EPS = 1e-8


def shared_mix(n, u):
    return sum(np.random.standard_normal((n, 1)) * u[r] for r in range(R))


def setup_inputs():
    u = np.random.standard_normal((R, D)) / np.sqrt(R)
    s = mx_kscale(D)
    r = (s / s.max())[np.arange(B) * D // B][:, None]
    current = (0.6 * shared_mix(B, u) + 0.45 * np.random.standard_normal((B, D))) * r
    memory = 2.4 * shared_mix(C, u) + 1.8 * np.random.standard_normal((C, D))
    return {"current": bf(current), "memory_matrix": bf(memory)}


def reference(current, memory_matrix):
    cur, mem = f64(current), f64(memory_matrix)
    mem_norm = np.maximum(np.sqrt((mem * mem).sum(-1)), EPS)
    cur_norm = np.maximum(np.sqrt((cur * cur).sum(-1, keepdims=True)), EPS)
    sim = (mxq(cur, 1, "e4m3") @ mxq(mem, 1, "e4m3").T) / (cur_norm * mem_norm[None, :])
    e = np.exp(sim - sim.max(-1, keepdims=True))
    attracted = (mxq(e, 1, "e4m3") @ mxq(mem, 0, "e4m3")) / e.sum(-1, keepdims=True)
    return 0.8 * attracted + 0.2 * cur

@@ -1,0 +1,375 @@
+from contextlib import ExitStack
+
+import concourse.mybir as mybir
+from concourse.masks import make_identity
+
+F32 = mybir.dt.float32
+BF16 = mybir.dt.bfloat16
+U32 = mybir.dt.uint32
+U8 = mybir.dt.uint8
+FP8X4 = mybir.dt.float8_e4m3fn_x4
+ALU = mybir.AluOpType
+ACT = mybir.ActivationFunctionType
+AX = mybir.AxisListType
+
+B, C, D = 256, 8192, 1024
+FLOPS = 2 * 2 * B * C * D
+EPS = 1e-8
+P = 128
+CH = 512
+NCH = C // CH
+NB = 3
+DEF = 3
+NBLK = NCH // 2
+PIN = True
+
+
+def tile_ca3_recurrentmatrix_pa_kernel(tc, current, memory_matrix, out):
+    nc = tc.nc
+    with ExitStack() as ctx:
+        if PIN:
+            ctx.enter_context(tc.manual_schedule())
+        keep = ctx.enter_context(tc.tile_pool(name="keep", bufs=1))
+        both = ctx.enter_context(tc.tile_pool(name="both", bufs=2))
+        psT = ctx.enter_context(tc.psum_pool(name="psT", bufs=4))
+        psD = ctx.enter_context(tc.psum_pool(name="psD", bufs=2))
+        psU = ctx.enter_context(tc.psum_pool(name="psU", bufs=2))
+
+        ident_f = keep.tile([P, P], F32, name="ident_f")
+        ident_b = keep.tile([P, P], BF16, name="ident_b")
+        codes2 = keep.tile([P, NCH, D], U32, name="codes2", align_bytes=64)
+        scales2 = keep.tile([P, NCH, D], U8, name="scales2", align_bytes=64)
+        sim = keep.tile([P, 2, C], F32, name="sim")
+        cur02 = keep.tile([P, 2, D], F32, name="cur02")
+        ccodes = keep.tile([P, 512], U32, name="ccodes", align_bytes=64)
+        cscales = keep.tile([P, 512], U8, name="cscales", align_bytes=64)
+        n2 = keep.tile([P, 4 * NCH], F32, name="n2")
+        nrm = keep.tile([P, 4 * NCH], F32, name="nrm")
+        nrmc = keep.tile([P, 4 * NCH], F32, name="nrmc")
+        rmn = keep.tile([P, 4 * NCH], F32, name="rmn")
+        cn2 = keep.tile([P, 2], F32, name="cn2")
+        cnrm = keep.tile([P, 2], F32, name="cnrm")
+        cnrmc = keep.tile([P, 2], F32, name="cnrmc")
+        rcn = keep.tile([P, 2], F32, name="rcn")
+        mx = keep.tile([P, 2, NCH], F32, name="mx")
+        mu = keep.tile([P, 2], F32, name="mu")
+        nb = keep.tile([P, 2], F32, name="nb")
+        rs = keep.tile([P, 2, NBLK], F32, name="rs")
+        rsum = keep.tile([P, 2], F32, name="rsum")
+        rinv = keep.tile([P, 2], F32, name="rinv")
+        wgt = keep.tile([P, 2], F32, name="wgt")
+        one = keep.tile([P, 1], F32, name="one")
+        one2 = keep.tile([P, 1], F32, name="one2")
+
+        nat = {}
+        g2 = {}
+
+        def load(i):
+            if i < NCH:
+                t = both.tile([P, 4, D], BF16, name="nat", tag="nat", bufs=NB)
+                nc.sync.dma_start(
+                    out=t[:], in_=memory_matrix[i * CH : (i + 1) * CH, :].rearrange("(p j) d -> p j d", j=4)
+                )
+                nat[i] = t
+
+        def regroup(i, h, eng):
+            t = both.tile([P, 512, 4], BF16, name="g2", tag="g2", bufs=2, align_bytes=64)
+            src = nat[i][:, :, h * 512 : (h + 1) * 512]
+            if eng == "v":
+                nc.vector.tensor_copy(
+                    out=t[:].rearrange("p (c i) t -> p c t i", i=4), in_=src.rearrange("p t (c i) -> p c t i", i=4)
+                )
+            else:
+                nc.scalar.copy(out=t[:], in_=src.rearrange("p t w -> p w t"))
+            g2[(i, h)] = t
+
+        def quant2(i, h):
+            nc.vector.quantize_mx(
+                out=codes2[:, i, h * 512 : (h + 1) * 512].bitcast(FP8X4),
+                scales=scales2[:, i, h * 512 : (h + 1) * 512],
+                in_=g2[(i, h)][:].rearrange("p w t -> p (w t)"),
+            )
+
+        with tc.tile_pool(name="pha", bufs=2) as pha:
+            nc.vector.memset(one[:], 1.0)
+            nc.scalar.sqrt(out=one2[:], in_=one[:])
+            make_identity(nc, ident_f[:])
+            make_identity(nc, ident_b[:])
+
+            curt = pha.tile([P, 2, D], BF16, name="curt", bufs=1)
+            nc.sync.dma_start(out=curt[:], in_=current.rearrange("(t p) d -> p t d", p=P))
+            for i in range(NB):
+                load(i)
+            junk = pha.tile([P, D], BF16, name="junk", bufs=1)
+
+            cur32 = curt[:].bitcast(F32)
+            gcur = pha.tile([P, 2048], BF16, name="gcur", bufs=1, align_bytes=64)
+            gcur32 = gcur[:].bitcast(F32)
+            for G in range(2):
+                bank = psT.tile([P, 512], F32, name="bankT", tag="T")
+                for u in range(2):
+                    for t in range(2):
+                        nc.tensor.transpose(
+                            bank[:, u * 256 + t * 128 : u * 256 + (t + 1) * 128],
+                            cur32[:, t, G * 256 + u * 128 : G * 256 + (u + 1) * 128],
+                            ident_f[:],
+                        )
+                nc.vector.tensor_copy(
+                    out=gcur32[:, G * 512 : (G + 1) * 512].rearrange("p (b u) -> p b u", u=2),
+                    in_=bank[:].rearrange("p (u b) -> p b u", u=2),
+                )
+            for t in range(2):
+                nc.scalar.activation(out=junk[:], in_=curt[:, t, :], func=ACT.Square, accum_out=cn2[:, t : t + 1])
+            nc.scalar.sqrt(out=cnrm[:], in_=cn2[:])
+            nc.vector.quantize_mx(out=ccodes[:].bitcast(FP8X4), scales=cscales[:], in_=gcur[:])
+            nc.vector.tensor_scalar_max(out=cnrmc[:], in0=cnrm[:], scalar1=EPS)
+            nc.vector.reciprocal(out=rcn[:], in_=cnrmc[:])
+            nc.gpsimd.tensor_scalar(out=cur02[:], in0=curt[:], scalar1=0.2, scalar2=0.0, op0=ALU.mult, op1=ALU.add)
+
+            g1 = {}
+            c1 = {}
+            s1 = {}
+            bD = {}
+            bU = {}
+            uTs = {}
+
+            def transposes(i):
+                late = i >= NCH - DEF
+                nat32 = nat[i][:].bitcast(F32)
+                for G in range(2):
+                    g = pha.tile([P, 2048], BF16, name="g1", tag="g1", bufs=2, align_bytes=64)
+                    g32 = g[:].bitcast(F32)
+                    for k in range(2):
+                        bank = psT.tile([P, 512], F32, name="bankT", tag="T")
+                        for jj in range(2):
+                            for u in range(2):
+                                nc.tensor.transpose(
+                                    bank[:, (jj * 2 + u) * 128 : (jj * 2 + u + 1) * 128],
+                                    nat32[:, 2 * k + jj, G * 256 + u * 128 : G * 256 + (u + 1) * 128],
+                                    ident_f[:],
+                                )
+                        dst = g32[:, k * 512 : (k + 1) * 512].rearrange("p (j c u) -> p j c u", j=2, u=2)
+                        src = bank[:].rearrange("p (j u c) -> p j c u", j=2, u=2)
+                        if late and (G, k) != (0, 0):
+                            nc.vector.tensor_copy(out=dst, in_=src)
+                        else:
+                            nc.scalar.copy(out=dst, in_=src)
+                    g1[(i, G)] = g
+
+            def norms(i):
+                for j in range(4):
+                    nc.scalar.activation(
+                        out=junk[:], in_=nat[i][:, j, :], func=ACT.Square, accum_out=n2[:, 4 * i + j : 4 * i + j + 1]
+                    )
+                nc.scalar.sqrt(out=nrm[:, 4 * i : 4 * i + 4], in_=n2[:, 4 * i : 4 * i + 4])
+
+            def recip(i):
+                nc.vector.tensor_scalar_max(out=nrmc[:, 4 * i : 4 * i + 4], in0=nrm[:, 4 * i : 4 * i + 4], scalar1=EPS)
+                nc.vector.reciprocal(out=rmn[:, 4 * i : 4 * i + 4], in_=nrmc[:, 4 * i : 4 * i + 4])
+
+            def quant1(i):
+                for G in range(2):
+                    c = pha.tile([P, 512], U32, name="c1", tag="c1", bufs=4, align_bytes=64)
+                    s = pha.tile([P, 512], U8, name="s1", tag="s1", bufs=4, align_bytes=64)
+                    nc.vector.quantize_mx(out=c[:].bitcast(FP8X4), scales=s[:], in_=g1[(i, G)][:])
+                    c1[(i, G)] = c
+                    s1[(i, G)] = s
+
+            def mm1(i):
+                for k in range(2):
+                    bank = psD.tile([P, 512], F32, name="bankD", tag="D")
+                    for jj in range(2):
+                        j = 2 * k + jj
+                        for G in range(2):
+                            nc.tensor.matmul_mx(
+                                out=bank[:, jj * 256 : (jj + 1) * 256],
+                                lhsT=c1[(i, G)][:, j * 128 : (j + 1) * 128].bitcast(FP8X4),
+                                lhsT_scale=s1[(i, G)][:, j * 128 : (j + 1) * 128],
+                                rhs=ccodes[:, G * 256 : (G + 1) * 256].bitcast(FP8X4),
+                                rhs_scale=cscales[:, G * 256 : (G + 1) * 256],
+                                start=(G == 0),
+                                stop=(G == 1),
+                            )
+                    bD[(i, k)] = bank
+
+            def evac1(i):
+                uT = pha.tile([P, 4, 256], F32, name="uT", tag="uT", bufs=2)
+                for k in range(2):
+                    nc.vector.tensor_tensor(
+                        out=uT[:, 2 * k : 2 * k + 2, :],
+                        in0=bD[(i, k)][:].rearrange("p (j b) -> p j b", j=2),
+                        in1=rmn[:, 4 * i + 2 * k : 4 * i + 2 * k + 2].unsqueeze(2).to_broadcast([P, 2, 256]),
+                        op=ALU.mult,
+                    )
+                uTs[i] = uT
+
+            def back(i):
+                for t in range(2):
+                    bank = psU.tile([P, 512], F32, name="bankU", tag="U")
+                    for j in range(4):
+                        nc.tensor.transpose(
+                            bank[:, j * 128 : (j + 1) * 128], uTs[i][:, j, t * 128 : (t + 1) * 128], ident_f[:]
+                        )
+                    bU[(i, t)] = bank
+
+            def evac2(i):
+                for t in range(2):
+                    nc.vector.tensor_scalar(
+                        out=sim[:, t, i * CH : (i + 1) * CH],
+                        in0=bU[(i, t)][:],
+                        scalar1=1.0,
+                        scalar2=None,
+                        op0=ALU.mult,
+                        op1=ALU.max,
+                        accum_out=mx[:, t, i : i + 1],
+                    )
+
+            for i in range(NCH + 1):
+                now = i < NCH
+                early = i < NCH - DEF
+                if now:
+                    transposes(i)
+                if i >= 1:
+                    evac1(i - 1)
+                    back(i - 1)
+                if now:
+                    norms(i)
+                if early:
+                    regroup(i, 0, "v")
+                    regroup(i, 1, "v")
+                if now:
+                    quant1(i)
+                    mm1(i)
+                if i >= 1:
+                    evac2(i - 1)
+                if early:
+                    quant2(i, 0)
+                    quant2(i, 1)
+                if now:
+                    recip(i)
+                if early:
+                    load(i + NB)
+            d0 = NCH - DEF
+            regroup(d0, 0, "s")
+            regroup(d0, 1, "s")
+
+        with tc.tile_pool(name="phb", bufs=2) as phb:
+            nc.vector.tensor_reduce(out=mu[:], in_=mx[:], axis=AX.X, op=ALU.max)
+            nc.vector.scalar_tensor_tensor(out=nb[:], in0=mu[:], scalar=-1.0, in1=rcn[:], op0=ALU.mult, op1=ALU.mult)
+
+            es = {}
+            bE = {}
+            ges = {}
+            ecs = {}
+            acc = [
+                [psD.tile([P, 512], F32, name="acc%d" % h, tag="D") for h in range(2)],
+                [psU.tile([P, 512], F32, name="acc%d" % (2 + h), tag="U") for h in range(2)],
+            ]
+
+            def expo(blk):
+                for t in range(2):
+                    e = phb.tile([P, 1024], BF16, name="e", tag="e", bufs=4)
+                    nc.scalar.activation(
+                        out=e[:],
+                        in_=sim[:, t, blk * 1024 : (blk + 1) * 1024],
+                        func=ACT.Exp,
+                        bias=nb[:, t : t + 1],
+                        scale=rcn[:, t : t + 1],
+                        accum_out=rs[:, t, blk : blk + 1],
+                    )
+                    es[(blk, t)] = e
+
+            def etrans(blk):
+                for gg in range(2):
+                    bank = psT.tile([P, 1024], BF16, name="bankE", tag="T")
+                    for T in range(4):
+                        for t in range(2):
+                            nc.tensor.transpose(
+                                bank[:, T * 256 + t * 128 : T * 256 + (t + 1) * 128],
+                                es[(blk, t)][:, gg * 512 + T * 128 : gg * 512 + (T + 1) * 128],
+                                ident_b[:],
+                            )
+                    bE[(blk, gg)] = bank
+
+            def evac3(blk):
+                ge = phb.tile([P, 2048], BF16, name="ge", tag="ge", bufs=3, align_bytes=64)
+                for gg in range(2):
+                    dst = ge[:, gg * 1024 : (gg + 1) * 1024].rearrange("p (b t) -> p b t", t=4)
+                    src = bE[(blk, gg)][:].rearrange("p (t b) -> p b t", t=4)
+                    if gg == 1 and blk % 2 == 0:
+                        nc.scalar.copy(out=dst, in_=src)
+                    else:
+                        nc.vector.tensor_copy(out=dst, in_=src)
+                ges[blk] = ge
+
+            def quante(blk):
+                c = phb.tile([P, 512], U32, name="ec", tag="ec", bufs=2, align_bytes=64)
+                s = phb.tile([P, 512], U8, name="esc", tag="esc", bufs=2, align_bytes=64)
+                nc.vector.quantize_mx(out=c[:].bitcast(FP8X4), scales=s[:], in_=ges[blk][:])
+                ecs[blk] = (c, s)
+
+            def mm2(blk):
+                c, s = ecs[blk]
+                for t in range(2):
+                    for gg in range(2):
+                        g = 2 * blk + gg
+                        lo = gg * 256 + t * 128
+                        for h in range(2):
+                            nc.tensor.matmul_mx(
+                                out=acc[t][h][:],
+                                lhsT=c[:, lo : lo + 128].bitcast(FP8X4),
+                                lhsT_scale=s[:, lo : lo + 128],
+                                rhs=codes2[:, g, h * 512 : (h + 1) * 512].bitcast(FP8X4),
+                                rhs_scale=scales2[:, g, h * 512 : (h + 1) * 512],
+                                start=(g == 0),
+                                stop=(g == NCH - 1),
+                            )
+
+            left = [("q", d0, 0), ("q", d0, 1)]
+            for i in range(d0 + 1, NCH):
+                left += [("r", i, 0), ("r", i, 1), ("q", i, 0), ("q", i, 1)]
+
+            done = [0]
+
+            def some_left(n):
+                for x in range(n):
+                    if done[0] < len(left):
+                        kind, i, h = left[done[0]]
+                        done[0] += 1
+                        if kind == "r":
+                            regroup(i, h, "v")
+                        else:
+                            quant2(i, h)
+
+            expo(0)
+            etrans(0)
+            some_left(4)
+            evac3(0)
+            expo(1)
+            etrans(1)
+            quante(0)
+            mm2(0)
+            evac3(1)
+            for blk in range(1, NBLK):
+                if blk + 1 < NBLK:
+                    expo(blk + 1)
+                    etrans(blk + 1)
+                    evac3(blk + 1)
+                some_left(2)
+                quante(blk)
+                mm2(blk)
+            nc.vector.tensor_reduce(out=rsum[:], in_=rs[:], axis=AX.X, op=ALU.add)
+            nc.vector.reciprocal(out=rinv[:], in_=rsum[:])
+            nc.vector.tensor_scalar_mul(out=wgt[:], in0=rinv[:], scalar1=0.8)
+            for t in range(2):
+                for h in range(2):
+                    o = phb.tile([P, 512], F32, name="o", tag="o", bufs=4)
+                    nc.vector.scalar_tensor_tensor(
+                        out=o[:],
+                        in0=acc[t][h][:],
+                        scalar=wgt[:, t : t + 1],
+                        in1=cur02[:, t, h * 512 : (h + 1) * 512],
+                        op0=ALU.mult,
+                        op1=ALU.add,
+                    )
+                    nc.sync.dma_start(out=out[t * P : (t + 1) * P, h * 512 : (h + 1) * 512], in_=o[:])

@@ -18,9 +18,14 @@ EPS = 1e-8
 P = 128
 CH = 512
 NCH = C // CH
-NB = 3
-DEF = 3
 NBLK = NCH // 2
+NB = 3
+DEF = 5
+SREG = 3
+FILL = [2, 2, 0]
+FILLB = [2, 2, 2, 2, 2, 2, 2, 2]
+SEV3 = [1, 2, 3, 4, 5, 6]
+VEVT = 3
 PIN = True
 
 
@@ -63,9 +68,12 @@ def tile_ca3_recurrentmatrix_pa_kernel(tc, current, memory_matrix, out):
 
         nat = {}
         g2 = {}
+        d0 = NCH - DEF
 
         def load(i):
-            if i < NCH:
+            if i < NCH + DEF:
+                if i >= NCH:
+                    i = i - DEF
                 t = both.tile([P, 4, D], BF16, name="nat", tag="nat", bufs=NB)
                 nc.sync.dma_start(
                     out=t[:], in_=memory_matrix[i * CH : (i + 1) * CH, :].rearrange("(p j) d -> p j d", j=4)
@@ -73,7 +81,7 @@ def tile_ca3_recurrentmatrix_pa_kernel(tc, current, memory_matrix, out):
                 nat[i] = t
 
         def regroup(i, h, eng):
-            t = both.tile([P, 512, 4], BF16, name="g2", tag="g2", bufs=2, align_bytes=64)
+            t = both.tile([P, 512, 4], BF16, name="g2", tag="g2", bufs=4, align_bytes=64)
             src = nat[i][:, :, h * 512 : (h + 1) * 512]
             if eng == "v":
                 nc.vector.tensor_copy(
@@ -90,55 +98,40 @@ def tile_ca3_recurrentmatrix_pa_kernel(tc, current, memory_matrix, out):
                 in_=g2[(i, h)][:].rearrange("p w t -> p (w t)"),
             )
 
+        halves = [(i, h) for i in range(d0, NCH) for h in range(2)]
+        left = [("q", i, h) for (i, h) in halves[:SREG]]
+        rest = halves[SREG:]
+        if len(rest) % 2:
+            left += [("r", rest[0][0], rest[0][1]), ("q", rest[0][0], rest[0][1])]
+            rest = rest[1:]
+        for x in range(0, len(rest), 2):
+            left += [("r", rest[x][0], rest[x][1]), ("r", rest[x + 1][0], rest[x + 1][1])]
+            left += [("q", rest[x][0], rest[x][1]), ("q", rest[x + 1][0], rest[x + 1][1])]
+        done = [0]
+
+        def some_left(n):
+            for x in range(n):
+                if done[0] < len(left):
+                    kind, i, h = left[done[0]]
+                    done[0] += 1
+                    if kind == "r":
+                        regroup(i, h, "v")
+                    else:
+                        quant2(i, h)
+
         with tc.tile_pool(name="pha", bufs=2) as pha:
-            nc.vector.memset(one[:], 1.0)
-            nc.scalar.sqrt(out=one2[:], in_=one[:])
-            make_identity(nc, ident_f[:])
-            make_identity(nc, ident_b[:])
-
-            curt = pha.tile([P, 2, D], BF16, name="curt", bufs=1)
-            nc.sync.dma_start(out=curt[:], in_=current.rearrange("(t p) d -> p t d", p=P))
-            for i in range(NB):
-                load(i)
-            junk = pha.tile([P, D], BF16, name="junk", bufs=1)
-
-            cur32 = curt[:].bitcast(F32)
-            gcur = pha.tile([P, 2048], BF16, name="gcur", bufs=1, align_bytes=64)
-            gcur32 = gcur[:].bitcast(F32)
-            for G in range(2):
-                bank = psT.tile([P, 512], F32, name="bankT", tag="T")
-                for u in range(2):
-                    for t in range(2):
-                        nc.tensor.transpose(
-                            bank[:, u * 256 + t * 128 : u * 256 + (t + 1) * 128],
-                            cur32[:, t, G * 256 + u * 128 : G * 256 + (u + 1) * 128],
-                            ident_f[:],
-                        )
-                nc.vector.tensor_copy(
-                    out=gcur32[:, G * 512 : (G + 1) * 512].rearrange("p (b u) -> p b u", u=2),
-                    in_=bank[:].rearrange("p (u b) -> p b u", u=2),
-                )
-            for t in range(2):
-                nc.scalar.activation(out=junk[:], in_=curt[:, t, :], func=ACT.Square, accum_out=cn2[:, t : t + 1])
-            nc.scalar.sqrt(out=cnrm[:], in_=cn2[:])
-            nc.vector.quantize_mx(out=ccodes[:].bitcast(FP8X4), scales=cscales[:], in_=gcur[:])
-            nc.vector.tensor_scalar_max(out=cnrmc[:], in0=cnrm[:], scalar1=EPS)
-            nc.vector.reciprocal(out=rcn[:], in_=cnrmc[:])
-            nc.gpsimd.tensor_scalar(out=cur02[:], in0=curt[:], scalar1=0.2, scalar2=0.0, op0=ALU.mult, op1=ALU.add)
-
             g1 = {}
             c1 = {}
             s1 = {}
+            bT = {}
             bD = {}
             bU = {}
             uTs = {}
+            junk = pha.tile([P, D], BF16, name="junk", bufs=1)
 
             def transposes(i):
-                late = i >= NCH - DEF
                 nat32 = nat[i][:].bitcast(F32)
                 for G in range(2):
-                    g = pha.tile([P, 2048], BF16, name="g1", tag="g1", bufs=2, align_bytes=64)
-                    g32 = g[:].bitcast(F32)
                     for k in range(2):
                         bank = psT.tile([P, 512], F32, name="bankT", tag="T")
                         for jj in range(2):
@@ -148,13 +141,22 @@ def tile_ca3_recurrentmatrix_pa_kernel(tc, current, memory_matrix, out):
                                     nat32[:, 2 * k + jj, G * 256 + u * 128 : G * 256 + (u + 1) * 128],
                                     ident_f[:],
                                 )
+                        bT[(i, G, k)] = bank
+
+            def evacT(i, eng):
+                nv = VEVT if i >= d0 else 0
+                for G in range(2):
+                    if (i, G) not in g1:
+                        g1[(i, G)] = pha.tile([P, 2048], BF16, name="g1", tag="g1", bufs=4, align_bytes=64)
+                    g32 = g1[(i, G)][:].bitcast(F32)
+                    for k in range(2):
                         dst = g32[:, k * 512 : (k + 1) * 512].rearrange("p (j c u) -> p j c u", j=2, u=2)
-                        src = bank[:].rearrange("p (j u c) -> p j c u", j=2, u=2)
-                        if late and (G, k) != (0, 0):
+                        src = bT[(i, G, k)][:].rearrange("p (j u c) -> p j c u", j=2, u=2)
+                        on_v = 2 * G + k >= 4 - nv
+                        if on_v and eng == "v":
                             nc.vector.tensor_copy(out=dst, in_=src)
-                        else:
+                        if not on_v and eng == "s":
                             nc.scalar.copy(out=dst, in_=src)
-                    g1[(i, G)] = g
 
             def norms(i):
                 for j in range(4):
@@ -169,8 +171,8 @@ def tile_ca3_recurrentmatrix_pa_kernel(tc, current, memory_matrix, out):
 
             def quant1(i):
                 for G in range(2):
-                    c = pha.tile([P, 512], U32, name="c1", tag="c1", bufs=4, align_bytes=64)
-                    s = pha.tile([P, 512], U8, name="s1", tag="s1", bufs=4, align_bytes=64)
+                    c = pha.tile([P, 512], U32, name="c1", tag="c1", bufs=2, align_bytes=64)
+                    s = pha.tile([P, 512], U8, name="s1", tag="s1", bufs=2, align_bytes=64)
                     nc.vector.quantize_mx(out=c[:].bitcast(FP8X4), scales=s[:], in_=g1[(i, G)][:])
                     c1[(i, G)] = c
                     s1[(i, G)] = s
@@ -224,34 +226,83 @@ def tile_ca3_recurrentmatrix_pa_kernel(tc, current, memory_matrix, out):
                         accum_out=mx[:, t, i : i + 1],
                     )
 
-            for i in range(NCH + 1):
-                now = i < NCH
-                early = i < NCH - DEF
-                if now:
+            nc.vector.memset(one[:], 1.0)
+            nc.scalar.sqrt(out=one2[:], in_=one[:])
+            make_identity(nc, ident_f[:])
+            make_identity(nc, ident_b[:])
+            load(0)
+            curt = pha.tile([P, 2, D], BF16, name="curt", tag="uT", bufs=2)
+            nc.sync.dma_start(out=curt[:], in_=current.rearrange("(t p) d -> p t d", p=P))
+            for i in range(1, NB):
+                load(i)
+
+            transposes(0)
+            evacT(0, "s")
+            regroup(0, 0, "v")
+            regroup(0, 1, "v")
+            quant2(0, 0)
+            quant2(0, 1)
+
+            cur32 = curt[:].bitcast(F32)
+            gcur = pha.tile([P, 2048], BF16, name="gcur", tag="g1", bufs=4, align_bytes=64)
+            gcur32 = gcur[:].bitcast(F32)
+            for G in range(2):
+                bank = psT.tile([P, 512], F32, name="bankT", tag="T")
+                for u in range(2):
+                    for t in range(2):
+                        nc.tensor.transpose(
+                            bank[:, u * 256 + t * 128 : u * 256 + (t + 1) * 128],
+                            cur32[:, t, G * 256 + u * 128 : G * 256 + (u + 1) * 128],
+                            ident_f[:],
+                        )
+                nc.vector.tensor_copy(
+                    out=gcur32[:, G * 512 : (G + 1) * 512].rearrange("p (b u) -> p b u", u=2),
+                    in_=bank[:].rearrange("p (u b) -> p b u", u=2),
+                )
+            norms(0)
+            load(NB)
+            for t in range(2):
+                nc.scalar.activation(out=junk[:], in_=curt[:, t, :], func=ACT.Square, accum_out=cn2[:, t : t + 1])
+            nc.scalar.sqrt(out=cnrm[:], in_=cn2[:])
+            nc.vector.quantize_mx(out=ccodes[:].bitcast(FP8X4), scales=cscales[:], in_=gcur[:])
+            nc.gpsimd.tensor_scalar(out=cur02[:], in0=curt[:], scalar1=0.2, scalar2=0.0, op0=ALU.mult, op1=ALU.add)
+
+            for i in range(1, NCH + 3):
+                if i < NCH:
                     transposes(i)
-                if i >= 1:
-                    evac1(i - 1)
-                    back(i - 1)
-                if now:
-                    norms(i)
-                if early:
+                if i == 1:
                     regroup(i, 0, "v")
                     regroup(i, 1, "v")
-                if now:
-                    quant1(i)
-                    mm1(i)
-                if i >= 1:
-                    evac2(i - 1)
-                if early:
                     quant2(i, 0)
                     quant2(i, 1)
-                if now:
-                    recip(i)
-                if early:
+                if 0 <= i - 3 < NCH:
+                    evac2(i - 3)
+                if 0 <= i - 2 < NCH:
+                    evac1(i - 2)
+                    back(i - 2)
+                if 0 <= i - 1 < NCH:
+                    recip(i - 1)
+                    quant1(i - 1)
+                    mm1(i - 1)
+                if i < NCH:
+                    norms(i)
+                    evacT(i, "s")
+                    evacT(i, "v")
+                if 1 < i < d0:
+                    regroup(i, 0, "v")
+                    regroup(i, 1, "v")
+                    quant2(i, 0)
+                    quant2(i, 1)
+                if i < NCH:
                     load(i + NB)
-            d0 = NCH - DEF
-            regroup(d0, 0, "s")
-            regroup(d0, 1, "s")
+                if i == 3:
+                    nc.vector.tensor_scalar_max(out=cnrmc[:], in0=cnrm[:], scalar1=EPS)
+                    nc.vector.reciprocal(out=rcn[:], in_=cnrmc[:])
+                if i == NCH:
+                    for x in range(SREG):
+                        regroup(halves[x][0], halves[x][1], "s")
+                if i >= NCH:
+                    some_left(FILL[i - NCH])
 
         with tc.tile_pool(name="phb", bufs=2) as phb:
             nc.vector.tensor_reduce(out=mu[:], in_=mx[:], axis=AX.X, op=ALU.max)
@@ -268,7 +319,7 @@ def tile_ca3_recurrentmatrix_pa_kernel(tc, current, memory_matrix, out):
 
             def expo(blk):
                 for t in range(2):
-                    e = phb.tile([P, 1024], BF16, name="e", tag="e", bufs=4)
+                    e = phb.tile([P, 1024], BF16, name="e", tag="e", bufs=6)
                     nc.scalar.activation(
                         out=e[:],
                         in_=sim[:, t, blk * 1024 : (blk + 1) * 1024],
@@ -292,11 +343,11 @@ def tile_ca3_recurrentmatrix_pa_kernel(tc, current, memory_matrix, out):
                     bE[(blk, gg)] = bank
 
             def evac3(blk):
-                ge = phb.tile([P, 2048], BF16, name="ge", tag="ge", bufs=3, align_bytes=64)
+                ge = phb.tile([P, 2048], BF16, name="ge", tag="ge", bufs=2, align_bytes=64)
                 for gg in range(2):
                     dst = ge[:, gg * 1024 : (gg + 1) * 1024].rearrange("p (b t) -> p b t", t=4)
                     src = bE[(blk, gg)][:].rearrange("p (t b) -> p b t", t=4)
-                    if gg == 1 and blk % 2 == 0:
+                    if gg == 1 and blk in SEV3:
                         nc.scalar.copy(out=dst, in_=src)
                     else:
                         nc.vector.tensor_copy(out=dst, in_=src)
@@ -325,39 +376,22 @@ def tile_ca3_recurrentmatrix_pa_kernel(tc, current, memory_matrix, out):
                                 stop=(g == NCH - 1),
                             )
 
-            left = [("q", d0, 0), ("q", d0, 1)]
-            for i in range(d0 + 1, NCH):
-                left += [("r", i, 0), ("r", i, 1), ("q", i, 0), ("q", i, 1)]
-
-            done = [0]
-
-            def some_left(n):
-                for x in range(n):
-                    if done[0] < len(left):
-                        kind, i, h = left[done[0]]
-                        done[0] += 1
-                        if kind == "r":
-                            regroup(i, h, "v")
-                        else:
-                            quant2(i, h)
-
             expo(0)
-            etrans(0)
-            some_left(4)
-            evac3(0)
             expo(1)
-            etrans(1)
+            etrans(0)
+            some_left(FILLB[0])
+            evac3(0)
             quante(0)
-            mm2(0)
-            evac3(1)
-            for blk in range(1, NBLK):
+            for blk in range(NBLK):
+                if blk + 2 < NBLK:
+                    expo(blk + 2)
                 if blk + 1 < NBLK:
-                    expo(blk + 1)
                     etrans(blk + 1)
-                    evac3(blk + 1)
-                some_left(2)
-                quante(blk)
                 mm2(blk)
+                if blk + 1 < NBLK:
+                    evac3(blk + 1)
+                    some_left(FILLB[blk + 1])
+                    quante(blk + 1)
             nc.vector.tensor_reduce(out=rsum[:], in_=rs[:], axis=AX.X, op=ALU.add)
             nc.vector.reciprocal(out=rinv[:], in_=rsum[:])
             nc.vector.tensor_scalar_mul(out=wgt[:], in0=rinv[:], scalar1=0.8)

@@ -22,10 +22,21 @@ NBLK = NCH // 2
 NB = 3
 DEF = 5
 SREG = 3
-FILL = [2, 2, 0]
-FILLB = [2, 2, 2, 2, 2, 2, 2, 2]
-SEV3 = [1, 2, 3, 4, 5, 6]
+FILL = [0, 0, 0, 0, 0, 0]
+FILLB = [4, 2, 2, 2, 2, 2, 2, 2]
+SEV3 = [0, 1, 2, 3, 4, 5, 6, 7]
 VEVT = 3
+GRAM = [0, 0, 0, 0, 0, 0, 0, 0, 0, 0, 0, 0, 0, 0, 0, 0]
+EV1V = [0, 1, 2, 3, 4, 5, 6, 7, 8, 9, 10, 11, 12, 13, 14, 15]
+SCHED = [
+    ("T", 0), ("ev2", 3), ("ev1", 2), ("back", 2), ("evT", 0), ("recip", 1), ("q1", 1), ("mm1", 1), ("norms", 0), ("evTs", 0),
+    ("rg", 0), ("q2", 0), ("rgg", -1), ("load", -3),
+]
+RUNOUT = [
+    ("ev1", 2), ("recip", 1), ("q1", 1), ("mm1", 1), ("ev2", 3), ("back", 2), ("load", -3),
+]
+GREG = [1, 2, 3, 4, 5, 6, 7, 8, 9, 10, 11, 12, 13, 14, 15]
+VEV = 1
 PIN = True
 
 
@@ -49,6 +60,8 @@ def tile_ca3_recurrentmatrix_pa_kernel(tc, current, memory_matrix, out):
         ccodes = keep.tile([P, 512], U32, name="ccodes", align_bytes=64)
         cscales = keep.tile([P, 512], U8, name="cscales", align_bytes=64)
         n2 = keep.tile([P, 4 * NCH], F32, name="n2")
+        n2g = keep.tile([P, 2 * NCH], F32, name="n2g")
+        junkf = keep.tile([P, P], F32, name="junkf")
         nrm = keep.tile([P, 4 * NCH], F32, name="nrm")
         nrmc = keep.tile([P, 4 * NCH], F32, name="nrmc")
         rmn = keep.tile([P, 4 * NCH], F32, name="rmn")
@@ -70,20 +83,30 @@ def tile_ca3_recurrentmatrix_pa_kernel(tc, current, memory_matrix, out):
         g2 = {}
         d0 = NCH - DEF
 
-        def load(i):
+        def load(i, first=False):
             if i < NCH + DEF:
                 if i >= NCH:
                     i = i - DEF
                 t = both.tile([P, 4, D], BF16, name="nat", tag="nat", bufs=NB)
-                nc.sync.dma_start(
-                    out=t[:], in_=memory_matrix[i * CH : (i + 1) * CH, :].rearrange("(p j) d -> p j d", j=4)
-                )
+                src = memory_matrix[i * CH : (i + 1) * CH, :].rearrange("(p j) d -> p j d", j=4)
+                if first:
+                    for j in range(4):
+                        nc.sync.dma_start(out=t[:, j : j + 1, :], in_=src[:, j : j + 1, :])
+                else:
+                    nc.sync.dma_start(out=t[:], in_=src)
                 nat[i] = t
 
         def regroup(i, h, eng):
-            t = both.tile([P, 512, 4], BF16, name="g2", tag="g2", bufs=4, align_bytes=64)
+            if eng == "g":
+                t = both.tile([P, 512, 4], BF16, name="g2g", tag="g2g", bufs=1, align_bytes=64)
+            else:
+                t = both.tile([P, 512, 4], BF16, name="g2", tag="g2", bufs=3, align_bytes=64)
             src = nat[i][:, :, h * 512 : (h + 1) * 512]
-            if eng == "v":
+            if eng == "g":
+                nc.gpsimd.tensor_scalar(
+                    out=t[:], in0=src.rearrange("p t w -> p w t"), scalar1=1.0, scalar2=0.0, op0=ALU.mult, op1=ALU.add
+                )
+            elif eng == "v":
                 nc.vector.tensor_copy(
                     out=t[:].rearrange("p (c i) t -> p c t i", i=4), in_=src.rearrange("p t (c i) -> p c t i", i=4)
                 )
@@ -91,7 +114,10 @@ def tile_ca3_recurrentmatrix_pa_kernel(tc, current, memory_matrix, out):
                 nc.scalar.copy(out=t[:], in_=src.rearrange("p t w -> p w t"))
             g2[(i, h)] = t
 
+        q2done = set()
+
         def quant2(i, h):
+            q2done.add((i, h))
             nc.vector.quantize_mx(
                 out=codes2[:, i, h * 512 : (h + 1) * 512].bitcast(FP8X4),
                 scales=scales2[:, i, h * 512 : (h + 1) * 512],
@@ -144,7 +170,7 @@ def tile_ca3_recurrentmatrix_pa_kernel(tc, current, memory_matrix, out):
                         bT[(i, G, k)] = bank
 
             def evacT(i, eng):
-                nv = VEVT if i >= d0 else 0
+                nv = VEVT if i >= d0 else VEV
                 for G in range(2):
                     if (i, G) not in g1:
                         g1[(i, G)] = pha.tile([P, 2048], BF16, name="g1", tag="g1", bufs=4, align_bytes=64)
@@ -158,12 +184,48 @@ def tile_ca3_recurrentmatrix_pa_kernel(tc, current, memory_matrix, out):
                         if not on_v and eng == "s":
                             nc.scalar.copy(out=dst, in_=src)
 
+            bG = {}
+
+            def gram(i):
+                if GRAM[i] == 0:
+                    return
+                bank = psT.tile([P, 512], F32, name="bankG", tag="T")
+                for j in range(GRAM[i]):
+                    for G in range(2):
+                        gv = g1[(i, G)][:].rearrange("p (c t) -> p c t", t=4)
+                        for t in range(4):
+                            nc.tensor.matmul(
+                                out=bank[:, j * 128 : (j + 1) * 128],
+                                lhsT=gv[:, j * 128 : (j + 1) * 128, t],
+                                rhs=gv[:, j * 128 : (j + 1) * 128, t],
+                                start=(G == 0 and t == 0),
+                                stop=(G == 1 and t == 3),
+                            )
+                bG[i] = bank
+
+            def diag(i):
+                for j in range(GRAM[i]):
+                    nc.vector.scalar_tensor_tensor(
+                        out=junkf[:],
+                        in0=bG[i][:, j * 128 : (j + 1) * 128],
+                        scalar=1.0,
+                        in1=ident_f[:],
+                        op0=ALU.mult,
+                        op1=ALU.mult,
+                        accum_out=n2g[:, 2 * i + j : 2 * i + j + 1],
+                    )
+
+            def sqrtg(i):
+                if GRAM[i] == 0:
+                    return
+                nc.scalar.sqrt(out=nrm[:, 4 * i : 4 * i + GRAM[i]], in_=n2g[:, 2 * i : 2 * i + GRAM[i]])
+
             def norms(i):
-                for j in range(4):
+                for j in range(GRAM[i], 4):
                     nc.scalar.activation(
                         out=junk[:], in_=nat[i][:, j, :], func=ACT.Square, accum_out=n2[:, 4 * i + j : 4 * i + j + 1]
                     )
-                nc.scalar.sqrt(out=nrm[:, 4 * i : 4 * i + 4], in_=n2[:, 4 * i : 4 * i + 4])
+                nc.scalar.sqrt(out=nrm[:, 4 * i + GRAM[i] : 4 * i + 4], in_=n2[:, 4 * i + GRAM[i] : 4 * i + 4])
 
             def recip(i):
                 nc.vector.tensor_scalar_max(out=nrmc[:, 4 * i : 4 * i + 4], in0=nrm[:, 4 * i : 4 * i + 4], scalar1=EPS)
@@ -196,18 +258,30 @@ def tile_ca3_recurrentmatrix_pa_kernel(tc, current, memory_matrix, out):
 
             def evac1(i):
                 uT = pha.tile([P, 4, 256], F32, name="uT", tag="uT", bufs=2)
-                for k in range(2):
-                    nc.vector.tensor_tensor(
-                        out=uT[:, 2 * k : 2 * k + 2, :],
-                        in0=bD[(i, k)][:].rearrange("p (j b) -> p j b", j=2),
-                        in1=rmn[:, 4 * i + 2 * k : 4 * i + 2 * k + 2].unsqueeze(2).to_broadcast([P, 2, 256]),
-                        op=ALU.mult,
-                    )
+                if i in EV1V:
+                    for k in range(2):
+                        nc.vector.tensor_tensor(
+                            out=uT[:, 2 * k : 2 * k + 2, :],
+                            in0=bD[(i, k)][:].rearrange("p (j b) -> p j b", j=2),
+                            in1=rmn[:, 4 * i + 2 * k : 4 * i + 2 * k + 2].unsqueeze(2).to_broadcast([P, 2, 256]),
+                            op=ALU.mult,
+                        )
+                else:
+                    for j in range(4):
+                        nc.scalar.activation(
+                            out=uT[:, j, :],
+                            in_=bD[(i, j // 2)][:, (j % 2) * 256 : (j % 2 + 1) * 256],
+                            func=ACT.Copy,
+                            scale=rmn[:, 4 * i + j : 4 * i + j + 1],
+                        )
                 uTs[i] = uT
 
             def back(i):
                 for t in range(2):
-                    bank = psU.tile([P, 512], F32, name="bankU", tag="U")
+                    if i == NCH - 1:
+                        bank = psT.tile([P, 512], F32, name="bankU2", tag="T")
+                    else:
+                        bank = psU.tile([P, 512], F32, name="bankU", tag="U")
                     for j in range(4):
                         nc.tensor.transpose(
                             bank[:, j * 128 : (j + 1) * 128], uTs[i][:, j, t * 128 : (t + 1) * 128], ident_f[:]
@@ -226,83 +300,92 @@ def tile_ca3_recurrentmatrix_pa_kernel(tc, current, memory_matrix, out):
                         accum_out=mx[:, t, i : i + 1],
                     )
 
+            def cur_path():
+                cur32 = curt[:].bitcast(F32)
+                gcur = pha.tile([P, 2048], BF16, name="gcur", tag="g1", bufs=4, align_bytes=64)
+                gcur32 = gcur[:].bitcast(F32)
+                for G in range(2):
+                    bank = psT.tile([P, 512], F32, name="bankT", tag="T")
+                    for u in range(2):
+                        for t in range(2):
+                            nc.tensor.transpose(
+                                bank[:, u * 256 + t * 128 : u * 256 + (t + 1) * 128],
+                                cur32[:, t, G * 256 + u * 128 : G * 256 + (u + 1) * 128],
+                                ident_f[:],
+                            )
+                    nc.vector.tensor_copy(
+                        out=gcur32[:, G * 512 : (G + 1) * 512].rearrange("p (b u) -> p b u", u=2),
+                        in_=bank[:].rearrange("p (u b) -> p b u", u=2),
+                    )
+                nc.vector.quantize_mx(out=ccodes[:].bitcast(FP8X4), scales=cscales[:], in_=gcur[:])
+                nc.gpsimd.tensor_scalar(out=cur02[:], in0=curt[:], scalar1=0.2, scalar2=0.0, op0=ALU.mult, op1=ALU.add)
+
+            def evT(i):
+                evacT(i, "v")
+
+            def evTs(i):
+                evacT(i, "s")
+
+            def rg(i):
+                if 0 < i < d0:
+                    if i not in GREG:
+                        regroup(i, 0, "v")
+                    regroup(i, 1, "v")
+
+            def rgg(i):
+                if i < d0 and i in GREG:
+                    regroup(i, 0, "g")
+
+            def q2(i):
+                if 0 < i < d0:
+                    quant2(i, 1)
+                    quant2(i, 0)
+
+            ops = {
+                "T": transposes, "evT": evT, "evTs": evTs, "gram": gram, "diag": diag, "sqrtg": sqrtg, "norms": norms,
+                "recip": recip, "q1": quant1, "mm1": mm1, "ev1": evac1, "back": back, "ev2": evac2, "rg": rg, "q2": q2, "rgg": rgg,
+            }
+
             nc.vector.memset(one[:], 1.0)
             nc.scalar.sqrt(out=one2[:], in_=one[:])
             make_identity(nc, ident_f[:])
             make_identity(nc, ident_b[:])
-            load(0)
+            load(0, True)
             curt = pha.tile([P, 2, D], BF16, name="curt", tag="uT", bufs=2)
             nc.sync.dma_start(out=curt[:], in_=current.rearrange("(t p) d -> p t d", p=P))
             for i in range(1, NB):
                 load(i)
 
-            transposes(0)
-            evacT(0, "s")
             regroup(0, 0, "v")
             regroup(0, 1, "v")
             quant2(0, 0)
             quant2(0, 1)
-
-            cur32 = curt[:].bitcast(F32)
-            gcur = pha.tile([P, 2048], BF16, name="gcur", tag="g1", bufs=4, align_bytes=64)
-            gcur32 = gcur[:].bitcast(F32)
-            for G in range(2):
-                bank = psT.tile([P, 512], F32, name="bankT", tag="T")
-                for u in range(2):
-                    for t in range(2):
-                        nc.tensor.transpose(
-                            bank[:, u * 256 + t * 128 : u * 256 + (t + 1) * 128],
-                            cur32[:, t, G * 256 + u * 128 : G * 256 + (u + 1) * 128],
-                            ident_f[:],
-                        )
-                nc.vector.tensor_copy(
-                    out=gcur32[:, G * 512 : (G + 1) * 512].rearrange("p (b u) -> p b u", u=2),
-                    in_=bank[:].rearrange("p (u b) -> p b u", u=2),
-                )
-            norms(0)
-            load(NB)
-            for t in range(2):
-                nc.scalar.activation(out=junk[:], in_=curt[:, t, :], func=ACT.Square, accum_out=cn2[:, t : t + 1])
-            nc.scalar.sqrt(out=cnrm[:], in_=cn2[:])
-            nc.vector.quantize_mx(out=ccodes[:].bitcast(FP8X4), scales=cscales[:], in_=gcur[:])
-            nc.gpsimd.tensor_scalar(out=cur02[:], in0=curt[:], scalar1=0.2, scalar2=0.0, op0=ALU.mult, op1=ALU.add)
-
-            for i in range(1, NCH + 3):
-                if i < NCH:
-                    transposes(i)
-                if i == 1:
-                    regroup(i, 0, "v")
-                    regroup(i, 1, "v")
-                    quant2(i, 0)
-                    quant2(i, 1)
-                if 0 <= i - 3 < NCH:
-                    evac2(i - 3)
-                if 0 <= i - 2 < NCH:
-                    evac1(i - 2)
-                    back(i - 2)
-                if 0 <= i - 1 < NCH:
-                    recip(i - 1)
-                    quant1(i - 1)
-                    mm1(i - 1)
-                if i < NCH:
-                    norms(i)
-                    evacT(i, "s")
-                    evacT(i, "v")
-                if 1 < i < d0:
-                    regroup(i, 0, "v")
-                    regroup(i, 1, "v")
-                    quant2(i, 0)
-                    quant2(i, 1)
-                if i < NCH:
-                    load(i + NB)
-                if i == 3:
-                    nc.vector.tensor_scalar_max(out=cnrmc[:], in0=cnrm[:], scalar1=EPS)
-                    nc.vector.reciprocal(out=rcn[:], in_=cnrmc[:])
+            last = max(lag for (op, lag) in SCHED)
+            for i in range(NCH + last + 1):
+                for op, lag in SCHED if i < NCH else RUNOUT:
+                    c = i - lag
+                    if op == "load":
+                        if NB <= c:
+                            load(c)
+                    elif 0 <= c < NCH:
+                        ops[op](c)
+                if i == 0:
+                    cur_path()
+                if i == d0:
+                    curt2 = both.tile([P, 2, D], BF16, name="curt2", tag="g2", bufs=3, align_bytes=64)
+                    nc.sync.dma_start(out=curt2[:], in_=current.rearrange("(t p) d -> p t d", p=P))
                 if i == NCH:
+                    for t in range(2):
+                        nc.scalar.activation(
+                            out=junk[:], in_=curt2[:, t, :], func=ACT.Square, accum_out=cn2[:, t : t + 1]
+                        )
+                    nc.scalar.sqrt(out=cnrm[:], in_=cn2[:])
                     for x in range(SREG):
                         regroup(halves[x][0], halves[x][1], "s")
                 if i >= NCH:
                     some_left(FILL[i - NCH])
+            nc.vector.tensor_scalar_max(out=cnrmc[:], in0=cnrm[:], scalar1=EPS)
+            nc.vector.reciprocal(out=rcn[:], in_=cnrmc[:])
 
         with tc.tile_pool(name="phb", bufs=2) as phb:
             nc.vector.tensor_reduce(out=mu[:], in_=mx[:], axis=AX.X, op=ALU.max)
@@ -387,6 +470,8 @@ def tile_ca3_recurrentmatrix_pa_kernel(tc, current, memory_matrix, out):
                     expo(blk + 2)
                 if blk + 1 < NBLK:
                     etrans(blk + 1)
+                while any((g, h) not in q2done for g in (2 * blk, 2 * blk + 1) for h in range(2)):
+                    some_left(1)
                 mm2(blk)
                 if blk + 1 < NBLK:
                     evac3(blk + 1)

@@ -20,8 +20,8 @@ CH = 512
 NCH = C // CH
 NBLK = NCH // 2
 NB = 3
-DEF = 5
-SREG = 3
+DEF = 8
+SREG = 1
 FILL = [0, 0, 0, 0, 0, 0]
 FILLB = [4, 2, 2, 2, 2, 2, 2, 2]
 SEV3 = [0, 1, 2, 3, 4, 5, 6, 7]
@@ -36,7 +36,10 @@ RUNOUT = [
     ("ev1", 2), ("recip", 1), ("q1", 1), ("mm1", 1), ("ev2", 3), ("back", 2), ("load", -3),
 ]
 GREG = [1, 2, 3, 4, 5, 6, 7, 8, 9, 10, 11, 12, 13, 14, 15]
-VEV = 1
+VEVL = [4, 1, 3, 1, 1, 1, 1, 1, 0, 3, 2, 2, 3, 2, 0, 0]
+KP = False
+VFIRST = False
+CB = 2
 PIN = True
 
 
@@ -124,7 +127,7 @@ def tile_ca3_recurrentmatrix_pa_kernel(tc, current, memory_matrix, out):
                 in_=g2[(i, h)][:].rearrange("p w t -> p (w t)"),
             )
 
-        halves = [(i, h) for i in range(d0, NCH) for h in range(2)]
+        halves = [(i, 1) for i in range(d0, NCH)]
         left = [("q", i, h) for (i, h) in halves[:SREG]]
         rest = halves[SREG:]
         if len(rest) % 2:
@@ -155,33 +158,41 @@ def tile_ca3_recurrentmatrix_pa_kernel(tc, current, memory_matrix, out):
             uTs = {}
             junk = pha.tile([P, D], BF16, name="junk", bufs=1)
 
-            def transposes(i):
+            def transposes(i, banks=(0, 1, 2, 3)):
                 nat32 = nat[i][:].bitcast(F32)
-                for G in range(2):
-                    for k in range(2):
-                        bank = psT.tile([P, 512], F32, name="bankT", tag="T")
-                        for jj in range(2):
-                            for u in range(2):
-                                nc.tensor.transpose(
-                                    bank[:, (jj * 2 + u) * 128 : (jj * 2 + u + 1) * 128],
-                                    nat32[:, 2 * k + jj, G * 256 + u * 128 : G * 256 + (u + 1) * 128],
-                                    ident_f[:],
-                                )
-                        bT[(i, G, k)] = bank
+                for b in banks:
+                    G, k = b // 2, b % 2
+                    bank = psT.tile([P, 512], F32, name="bankT", tag="T")
+                    for jj in range(2):
+                        for u in range(2):
+                            nc.tensor.transpose(
+                                bank[:, (jj * 2 + u) * 128 : (jj * 2 + u + 1) * 128],
+                                nat32[:, 2 * k + jj, G * 256 + u * 128 : G * 256 + (u + 1) * 128],
+                                ident_f[:],
+                            )
+                    bT[(i, G, k)] = bank
+
+            def t_a(i):
+                transposes(i, (0, 1, 2))
+
+            def t_b(i):
+                transposes(i, (3,))
 
             def evacT(i, eng):
-                nv = VEVT if i >= d0 else VEV
+                nv = VEVL[i]
                 for G in range(2):
                     if (i, G) not in g1:
                         g1[(i, G)] = pha.tile([P, 2048], BF16, name="g1", tag="g1", bufs=4, align_bytes=64)
                     g32 = g1[(i, G)][:].bitcast(F32)
                     for k in range(2):
+                        on_v = (2 * G + k < nv) if VFIRST else (2 * G + k >= 4 - nv)
+                        if on_v != (eng == "v"):
+                            continue
                         dst = g32[:, k * 512 : (k + 1) * 512].rearrange("p (j c u) -> p j c u", j=2, u=2)
                         src = bT[(i, G, k)][:].rearrange("p (j u c) -> p j c u", j=2, u=2)
-                        on_v = 2 * G + k >= 4 - nv
-                        if on_v and eng == "v":
+                        if on_v:
                             nc.vector.tensor_copy(out=dst, in_=src)
-                        if not on_v and eng == "s":
+                        else:
                             nc.scalar.copy(out=dst, in_=src)
 
             bG = {}
@@ -233,8 +244,8 @@ def tile_ca3_recurrentmatrix_pa_kernel(tc, current, memory_matrix, out):
 
             def quant1(i):
                 for G in range(2):
-                    c = pha.tile([P, 512], U32, name="c1", tag="c1", bufs=2, align_bytes=64)
-                    s = pha.tile([P, 512], U8, name="s1", tag="s1", bufs=2, align_bytes=64)
+                    c = pha.tile([P, 512], U32, name="c1", tag="c1", bufs=CB, align_bytes=64)
+                    s = pha.tile([P, 512], U8, name="s1", tag="s1", bufs=CB, align_bytes=64)
                     nc.vector.quantize_mx(out=c[:].bitcast(FP8X4), scales=s[:], in_=g1[(i, G)][:])
                     c1[(i, G)] = c
                     s1[(i, G)] = s
@@ -318,7 +329,6 @@ def tile_ca3_recurrentmatrix_pa_kernel(tc, current, memory_matrix, out):
                         in_=bank[:].rearrange("p (u b) -> p b u", u=2),
                     )
                 nc.vector.quantize_mx(out=ccodes[:].bitcast(FP8X4), scales=cscales[:], in_=gcur[:])
-                nc.gpsimd.tensor_scalar(out=cur02[:], in0=curt[:], scalar1=0.2, scalar2=0.0, op0=ALU.mult, op1=ALU.add)
 
             def evT(i):
                 evacT(i, "v")
@@ -333,16 +343,17 @@ def tile_ca3_recurrentmatrix_pa_kernel(tc, current, memory_matrix, out):
                     regroup(i, 1, "v")
 
             def rgg(i):
-                if i < d0 and i in GREG:
+                if i in GREG:
                     regroup(i, 0, "g")
 
             def q2(i):
                 if 0 < i < d0:
                     quant2(i, 1)
+                if 0 < i:
                     quant2(i, 0)
 
             ops = {
-                "T": transposes, "evT": evT, "evTs": evTs, "gram": gram, "diag": diag, "sqrtg": sqrtg, "norms": norms,
+                "T": transposes, "TA": t_a, "TB": t_b, "evT": evT, "evTs": evTs, "gram": gram, "diag": diag, "sqrtg": sqrtg, "norms": norms,
                 "recip": recip, "q1": quant1, "mm1": mm1, "ev1": evac1, "back": back, "ev2": evac2, "rg": rg, "q2": q2, "rgg": rgg,
             }
 
@@ -380,10 +391,15 @@ def tile_ca3_recurrentmatrix_pa_kernel(tc, current, memory_matrix, out):
                             out=junk[:], in_=curt2[:, t, :], func=ACT.Square, accum_out=cn2[:, t : t + 1]
                         )
                     nc.scalar.sqrt(out=cnrm[:], in_=cn2[:])
+                    nc.gpsimd.tensor_scalar(
+                        out=cur02[:], in0=curt2[:], scalar1=0.2, scalar2=0.0, op0=ALU.mult, op1=ALU.add
+                    )
                     for x in range(SREG):
                         regroup(halves[x][0], halves[x][1], "s")
                 if i >= NCH:
                     some_left(FILL[i - NCH])
+            for c in range(NCH + last + 1 + NB, NCH + DEF):
+                load(c)
             nc.vector.tensor_scalar_max(out=cnrmc[:], in0=cnrm[:], scalar1=EPS)
             nc.vector.reciprocal(out=rcn[:], in_=cnrmc[:])
 
@@ -416,20 +432,34 @@ def tile_ca3_recurrentmatrix_pa_kernel(tc, current, memory_matrix, out):
             def etrans(blk):
                 for gg in range(2):
                     bank = psT.tile([P, 1024], BF16, name="bankE", tag="T")
+                    bv = bank[:].rearrange("p (b t) -> p b t", t=4)
                     for T in range(4):
                         for t in range(2):
-                            nc.tensor.transpose(
-                                bank[:, T * 256 + t * 128 : T * 256 + (t + 1) * 128],
-                                es[(blk, t)][:, gg * 512 + T * 128 : gg * 512 + (T + 1) * 128],
-                                ident_b[:],
-                            )
+                            if KP:
+                                nc.tensor.matmul(
+                                    out=bv[:, t * 128 : (t + 1) * 128, T],
+                                    lhsT=es[(blk, t)][:, gg * 512 + T * 128 : gg * 512 + (T + 1) * 128],
+                                    rhs=ident_b[:],
+                                    start=True,
+                                    stop=True,
+                                )
+                            else:
+                                nc.tensor.transpose(
+                                    bank[:, T * 256 + t * 128 : T * 256 + (t + 1) * 128],
+                                    es[(blk, t)][:, gg * 512 + T * 128 : gg * 512 + (T + 1) * 128],
+                                    ident_b[:],
+                                )
                     bE[(blk, gg)] = bank
 
             def evac3(blk):
                 ge = phb.tile([P, 2048], BF16, name="ge", tag="ge", bufs=2, align_bytes=64)
                 for gg in range(2):
-                    dst = ge[:, gg * 1024 : (gg + 1) * 1024].rearrange("p (b t) -> p b t", t=4)
-                    src = bE[(blk, gg)][:].rearrange("p (t b) -> p b t", t=4)
+                    if KP:
+                        dst = ge[:, gg * 1024 : (gg + 1) * 1024]
+                        src = bE[(blk, gg)][:]
+                    else:
+                        dst = ge[:, gg * 1024 : (gg + 1) * 1024].rearrange("p (b t) -> p b t", t=4)
+                        src = bE[(blk, gg)][:].rearrange("p (t b) -> p b t", t=4)
                     if gg == 1 and blk in SEV3:
                         nc.scalar.copy(out=dst, in_=src)
                     else:

@@ -20,26 +20,21 @@ CH = 512
 NCH = C // CH
 NBLK = NCH // 2
 NB = 3
-DEF = 8
+DEF = 9
 SREG = 1
-FILL = [0, 0, 0, 0, 0, 0]
+FILL = [0, 0, 0, 0, 0, 0, 0, 0]
 FILLB = [4, 2, 2, 2, 2, 2, 2, 2]
-SEV3 = [0, 1, 2, 3, 4, 5, 6, 7]
+SEV3 = [1, 2, 3, 4, 5, 6, 7]
 VEVT = 3
-GRAM = [0, 0, 0, 0, 0, 0, 0, 0, 0, 0, 0, 0, 0, 0, 0, 0]
-EV1V = [0, 1, 2, 3, 4, 5, 6, 7, 8, 9, 10, 11, 12, 13, 14, 15]
-SCHED = [
-    ("T", 0), ("ev2", 3), ("ev1", 2), ("back", 2), ("evT", 0), ("recip", 1), ("q1", 1), ("mm1", 1), ("norms", 0), ("evTs", 0),
-    ("rg", 0), ("q2", 0), ("rgg", -1), ("load", -3),
-]
-RUNOUT = [
-    ("ev1", 2), ("recip", 1), ("q1", 1), ("mm1", 1), ("ev2", 3), ("back", 2), ("load", -3),
-]
+GRAM = [1, 2, 0, 2, 2, 2, 1, 2, 1, 2, 0, 0, 0, 2, 2, 0]
+EV1V = [5, 7, 8, 9, 10, 11, 12, 14]
+SCHED = [("ev1", 3), ("TA", 0), ("evT", 0), ("ev2", 4), ("TB", 0), ("rg", 0), ("q2", 0), ("mm1", 2), ("q1", 1), ("gram", 1), ("evTs", 0), ("rgg", -1), ("norms", 0), ("diag", 1), ("sqrtg", 1), ("recip", 1), ("load", -3), ("back", 3)]
+RUNOUT = [("ev1", 3), ("gram", 1), ("q1", 1), ("diag", 1), ("sqrtg", 1), ("recip", 1), ("mm1", 2), ("ev2", 4), ("back", 3), ("load", -3)]
 GREG = [1, 2, 3, 4, 5, 6, 7, 8, 9, 10, 11, 12, 13, 14, 15]
-VEVL = [4, 1, 3, 1, 1, 1, 1, 1, 0, 3, 2, 2, 3, 2, 0, 0]
+VEVL = [1, 0, 1, 1, 1, 0, 1, 2, 0, 2, 2, 1, 1, 0, 2, 2]
 KP = False
-VFIRST = False
-CB = 2
+VFIRST = True
+CB = 4
 PIN = True
 
 

@@ -23,26 +23,18 @@ NB = 3
 DEF = 9
 SREG = 1
 FILL = [0, 0, 0, 0, 0, 0, 0, 0]
-FILLB = [4, 2, 2, 2, 2, 2, 2, 2]
+FILLB = [4, 3, 1, 2, 2, 2, 2, 2]
 SEV3 = [1, 2, 3, 4, 5, 6, 7]
-VEVT = 3
-GRAM = [1, 2, 0, 2, 2, 2, 1, 2, 1, 2, 0, 0, 0, 2, 2, 0]
-EV1V = [5, 7, 8, 9, 10, 11, 12, 14]
-SCHED = [("ev1", 3), ("TA", 0), ("evT", 0), ("ev2", 4), ("TB", 0), ("rg", 0), ("q2", 0), ("mm1", 2), ("q1", 1), ("gram", 1), ("evTs", 0), ("rgg", -1), ("norms", 0), ("diag", 1), ("sqrtg", 1), ("recip", 1), ("load", -3), ("back", 3)]
-RUNOUT = [("ev1", 3), ("gram", 1), ("q1", 1), ("diag", 1), ("sqrtg", 1), ("recip", 1), ("mm1", 2), ("ev2", 4), ("back", 3), ("load", -3)]
-GREG = [1, 2, 3, 4, 5, 6, 7, 8, 9, 10, 11, 12, 13, 14, 15]
-VEVL = [1, 0, 1, 1, 1, 0, 1, 2, 0, 2, 2, 1, 1, 0, 2, 2]
-KP = False
-VFIRST = True
-CB = 4
-PIN = True
+VEVL = [4, 2, 4, 2, 1, 0, 2, 1, 0, 3, 2, 2, 4, 4, 0, 1]
+EXPG = [(0, 2), (2, 2), (4, 2), (6, 2), (8, 2), (10, 2), (12, 2), (14, 2)]
+SCHED = [("T", 0), ("ev2", 3), ("ev1", 2), ("back", 2), ("evTs", 0), ("q1", 1), ("mm1", 1), ("rg", 0), ("q2", 0), ("evT", 0), ("rgg", -1), ("load", -3), ("norms", -1), ("recip", 0)]
+RUNOUT = [("ev1", 2), ("q1", 1), ("mm1", 1), ("ev2", 3), ("back", 2), ("load", -3)]
 
 
 def tile_ca3_recurrentmatrix_pa_kernel(tc, current, memory_matrix, out):
     nc = tc.nc
     with ExitStack() as ctx:
-        if PIN:
-            ctx.enter_context(tc.manual_schedule())
+        ctx.enter_context(tc.manual_schedule())
         keep = ctx.enter_context(tc.tile_pool(name="keep", bufs=1))
         both = ctx.enter_context(tc.tile_pool(name="both", bufs=2))
         psT = ctx.enter_context(tc.psum_pool(name="psT", bufs=4))
@@ -58,9 +50,7 @@ def tile_ca3_recurrentmatrix_pa_kernel(tc, current, memory_matrix, out):
         ccodes = keep.tile([P, 512], U32, name="ccodes", align_bytes=64)
         cscales = keep.tile([P, 512], U8, name="cscales", align_bytes=64)
         n2 = keep.tile([P, 4 * NCH], F32, name="n2")
-        n2g = keep.tile([P, 2 * NCH], F32, name="n2g")
-        junkf = keep.tile([P, P], F32, name="junkf")
-        nrm = keep.tile([P, 4 * NCH], F32, name="nrm")
+        nrm = keep.tile([P, 4 * NCH, 2], F32, name="nrm")
         nrmc = keep.tile([P, 4 * NCH], F32, name="nrmc")
         rmn = keep.tile([P, 4 * NCH], F32, name="rmn")
         cn2 = keep.tile([P, 2], F32, name="cn2")
@@ -70,7 +60,7 @@ def tile_ca3_recurrentmatrix_pa_kernel(tc, current, memory_matrix, out):
         mx = keep.tile([P, 2, NCH], F32, name="mx")
         mu = keep.tile([P, 2], F32, name="mu")
         nb = keep.tile([P, 2], F32, name="nb")
-        rs = keep.tile([P, 2, NBLK], F32, name="rs")
+        rs = keep.tile([P, 2, len(EXPG)], F32, name="rs")
         rsum = keep.tile([P, 2], F32, name="rsum")
         rinv = keep.tile([P, 2], F32, name="rinv")
         wgt = keep.tile([P, 2], F32, name="wgt")
@@ -78,8 +68,10 @@ def tile_ca3_recurrentmatrix_pa_kernel(tc, current, memory_matrix, out):
         one2 = keep.tile([P, 1], F32, name="one2")
 
         nat = {}
-        g2 = {}
+        g2w = {}
+        g2h = {}
         d0 = NCH - DEF
+        q2done = set()
 
         def load(i, first=False):
             if i < NCH + DEF:
@@ -94,68 +86,86 @@ def tile_ca3_recurrentmatrix_pa_kernel(tc, current, memory_matrix, out):
                     nc.sync.dma_start(out=t[:], in_=src)
                 nat[i] = t
 
-        def regroup(i, h, eng):
-            if eng == "g":
-                t = both.tile([P, 512, 4], BF16, name="g2g", tag="g2g", bufs=1, align_bytes=64)
-            else:
-                t = both.tile([P, 512, 4], BF16, name="g2", tag="g2", bufs=3, align_bytes=64)
-            src = nat[i][:, :, h * 512 : (h + 1) * 512]
-            if eng == "g":
-                nc.gpsimd.tensor_scalar(
-                    out=t[:], in0=src.rearrange("p t w -> p w t"), scalar1=1.0, scalar2=0.0, op0=ALU.mult, op1=ALU.add
-                )
-            elif eng == "v":
-                nc.vector.tensor_copy(
-                    out=t[:].rearrange("p (c i) t -> p c t i", i=4), in_=src.rearrange("p t (c i) -> p c t i", i=4)
-                )
-            else:
-                nc.scalar.copy(out=t[:], in_=src.rearrange("p t w -> p w t"))
-            g2[(i, h)] = t
-
-        q2done = set()
-
-        def quant2(i, h):
-            q2done.add((i, h))
-            nc.vector.quantize_mx(
-                out=codes2[:, i, h * 512 : (h + 1) * 512].bitcast(FP8X4),
-                scales=scales2[:, i, h * 512 : (h + 1) * 512],
-                in_=g2[(i, h)][:].rearrange("p w t -> p (w t)"),
+        def vcopy(dst, src):
+            nc.vector.tensor_copy(
+                out=dst.rearrange("p (c i) t -> p c t i", i=4), in_=src.rearrange("p t (c i) -> p c t i", i=4)
             )
 
-        halves = [(i, 1) for i in range(d0, NCH)]
-        left = [("q", i, h) for (i, h) in halves[:SREG]]
-        rest = halves[SREG:]
-        if len(rest) % 2:
-            left += [("r", rest[0][0], rest[0][1]), ("q", rest[0][0], rest[0][1])]
-            rest = rest[1:]
-        for x in range(0, len(rest), 2):
-            left += [("r", rest[x][0], rest[x][1]), ("r", rest[x + 1][0], rest[x + 1][1])]
-            left += [("q", rest[x][0], rest[x][1]), ("q", rest[x + 1][0], rest[x + 1][1])]
+        def whole(i):
+            g2w[i] = both.tile([P, D, 4], BF16, name="g2w", tag="g2w", bufs=1, align_bytes=64)
+
+        def rgg(i):
+            whole(i)
+            nc.gpsimd.tensor_scalar(
+                out=g2w[i][:, :512, :],
+                in0=nat[i][:, :, :512].rearrange("p t w -> p w t"),
+                scalar1=1.0,
+                scalar2=0.0,
+                op0=ALU.mult,
+                op1=ALU.add,
+            )
+
+        def rg(i):
+            if 0 < i < d0:
+                vcopy(g2w[i][:, 512:, :], nat[i][:, :, 512:])
+
+        def q2(i):
+            if i == 0:
+                return
+            w = D if i < d0 else 512
+            nc.vector.quantize_mx(
+                out=codes2[:, i, :w].bitcast(FP8X4),
+                scales=scales2[:, i, :w],
+                in_=g2w[i][:, :w, :].rearrange("p w t -> p (w t)"),
+            )
+            q2done.add((i, 0))
+            if i < d0:
+                q2done.add((i, 1))
+
+        def regroup_half(i, eng):
+            t = both.tile([P, 512, 4], BF16, name="g2h", tag="g2h", bufs=2, align_bytes=64)
+            if eng == "v":
+                vcopy(t[:], nat[i][:, :, 512:])
+            else:
+                nc.scalar.copy(out=t[:], in_=nat[i][:, :, 512:].rearrange("p t w -> p w t"))
+            g2h[i] = t
+
+        def quant_half(i):
+            q2done.add((i, 1))
+            nc.vector.quantize_mx(
+                out=codes2[:, i, 512:].bitcast(FP8X4),
+                scales=scales2[:, i, 512:],
+                in_=g2h[i][:].rearrange("p w t -> p (w t)"),
+            )
+
+        late = list(range(d0, NCH))
+        left = [("q", i) for i in late[:SREG]]
+        for i in late[SREG:]:
+            left += [("r", i), ("q", i)]
         done = [0]
 
         def some_left(n):
             for x in range(n):
                 if done[0] < len(left):
-                    kind, i, h = left[done[0]]
+                    kind, i = left[done[0]]
                     done[0] += 1
                     if kind == "r":
-                        regroup(i, h, "v")
+                        regroup_half(i, "v")
                     else:
-                        quant2(i, h)
+                        quant_half(i)
 
         with tc.tile_pool(name="pha", bufs=2) as pha:
             g1 = {}
             c1 = {}
-            s1 = {}
             bT = {}
             bD = {}
             bU = {}
             uTs = {}
             junk = pha.tile([P, D], BF16, name="junk", bufs=1)
 
-            def transposes(i, banks=(0, 1, 2, 3)):
+            def transposes(i):
                 nat32 = nat[i][:].bitcast(F32)
-                for b in banks:
+                for b in range(4):
                     G, k = b // 2, b % 2
                     bank = psT.tile([P, 512], F32, name="bankT", tag="T")
                     for jj in range(2):
@@ -165,96 +175,61 @@ def tile_ca3_recurrentmatrix_pa_kernel(tc, current, memory_matrix, out):
                                 nat32[:, 2 * k + jj, G * 256 + u * 128 : G * 256 + (u + 1) * 128],
                                 ident_f[:],
                             )
-                    bT[(i, G, k)] = bank
+                    bT[(i, b)] = bank
 
-            def t_a(i):
-                transposes(i, (0, 1, 2))
+            def evac_t(i, eng):
+                if i not in g1:
+                    g1[i] = pha.tile([P, 4096], BF16, name="g1", tag="g1", bufs=2, align_bytes=64)
+                g32 = g1[i][:].bitcast(F32)
+                for b in range(4):
+                    on_v = b >= 4 - VEVL[i]
+                    if on_v != (eng == "v"):
+                        continue
+                    dst = g32[:, b * 512 : (b + 1) * 512].rearrange("p (j c u) -> p j c u", j=2, u=2)
+                    src = bT[(i, b)][:].rearrange("p (j u c) -> p j c u", j=2, u=2)
+                    if on_v:
+                        nc.vector.tensor_copy(out=dst, in_=src)
+                    else:
+                        nc.scalar.copy(out=dst, in_=src)
 
-            def t_b(i):
-                transposes(i, (3,))
+            def ev_v(i):
+                evac_t(i, "v")
 
-            def evacT(i, eng):
-                nv = VEVL[i]
-                for G in range(2):
-                    if (i, G) not in g1:
-                        g1[(i, G)] = pha.tile([P, 2048], BF16, name="g1", tag="g1", bufs=4, align_bytes=64)
-                    g32 = g1[(i, G)][:].bitcast(F32)
-                    for k in range(2):
-                        on_v = (2 * G + k < nv) if VFIRST else (2 * G + k >= 4 - nv)
-                        if on_v != (eng == "v"):
-                            continue
-                        dst = g32[:, k * 512 : (k + 1) * 512].rearrange("p (j c u) -> p j c u", j=2, u=2)
-                        src = bT[(i, G, k)][:].rearrange("p (j u c) -> p j c u", j=2, u=2)
-                        if on_v:
-                            nc.vector.tensor_copy(out=dst, in_=src)
-                        else:
-                            nc.scalar.copy(out=dst, in_=src)
-
-            bG = {}
-
-            def gram(i):
-                if GRAM[i] == 0:
-                    return
-                bank = psT.tile([P, 512], F32, name="bankG", tag="T")
-                for j in range(GRAM[i]):
-                    for G in range(2):
-                        gv = g1[(i, G)][:].rearrange("p (c t) -> p c t", t=4)
-                        for t in range(4):
-                            nc.tensor.matmul(
-                                out=bank[:, j * 128 : (j + 1) * 128],
-                                lhsT=gv[:, j * 128 : (j + 1) * 128, t],
-                                rhs=gv[:, j * 128 : (j + 1) * 128, t],
-                                start=(G == 0 and t == 0),
-                                stop=(G == 1 and t == 3),
-                            )
-                bG[i] = bank
-
-            def diag(i):
-                for j in range(GRAM[i]):
-                    nc.vector.scalar_tensor_tensor(
-                        out=junkf[:],
-                        in0=bG[i][:, j * 128 : (j + 1) * 128],
-                        scalar=1.0,
-                        in1=ident_f[:],
-                        op0=ALU.mult,
-                        op1=ALU.mult,
-                        accum_out=n2g[:, 2 * i + j : 2 * i + j + 1],
-                    )
-
-            def sqrtg(i):
-                if GRAM[i] == 0:
-                    return
-                nc.scalar.sqrt(out=nrm[:, 4 * i : 4 * i + GRAM[i]], in_=n2g[:, 2 * i : 2 * i + GRAM[i]])
+            def ev_s(i):
+                evac_t(i, "s")
 
             def norms(i):
-                for j in range(GRAM[i], 4):
+                for j in range(4):
                     nc.scalar.activation(
                         out=junk[:], in_=nat[i][:, j, :], func=ACT.Square, accum_out=n2[:, 4 * i + j : 4 * i + j + 1]
                     )
-                nc.scalar.sqrt(out=nrm[:, 4 * i + GRAM[i] : 4 * i + 4], in_=n2[:, 4 * i + GRAM[i] : 4 * i + 4])
+                if i % 2:
+                    nc.scalar.sqrt(out=nrm[:, 4 * i - 4 : 4 * i + 4, 0], in_=n2[:, 4 * i - 4 : 4 * i + 4])
 
             def recip(i):
-                nc.vector.tensor_scalar_max(out=nrmc[:, 4 * i : 4 * i + 4], in0=nrm[:, 4 * i : 4 * i + 4], scalar1=EPS)
-                nc.vector.reciprocal(out=rmn[:, 4 * i : 4 * i + 4], in_=nrmc[:, 4 * i : 4 * i + 4])
+                if i % 2:
+                    nc.vector.tensor_reduce(
+                        out=nrmc[:, 4 * i - 4 : 4 * i + 4], in_=nrm[:, 4 * i - 4 : 4 * i + 4, :], axis=AX.X, op=ALU.max
+                    )
+                    nc.vector.reciprocal(out=rmn[:, 4 * i - 4 : 4 * i + 4], in_=nrmc[:, 4 * i - 4 : 4 * i + 4])
 
             def quant1(i):
-                for G in range(2):
-                    c = pha.tile([P, 512], U32, name="c1", tag="c1", bufs=CB, align_bytes=64)
-                    s = pha.tile([P, 512], U8, name="s1", tag="s1", bufs=CB, align_bytes=64)
-                    nc.vector.quantize_mx(out=c[:].bitcast(FP8X4), scales=s[:], in_=g1[(i, G)][:])
-                    c1[(i, G)] = c
-                    s1[(i, G)] = s
+                c = pha.tile([P, 1024], U32, name="c1", tag="c1", bufs=1, align_bytes=64)
+                s = pha.tile([P, 1024], U8, name="s1", tag="s1", bufs=1, align_bytes=64)
+                nc.vector.quantize_mx(out=c[:].bitcast(FP8X4), scales=s[:], in_=g1[i][:])
+                c1[i] = (c, s)
 
             def mm1(i):
+                c, s = c1[i]
                 for k in range(2):
                     bank = psD.tile([P, 512], F32, name="bankD", tag="D")
                     for jj in range(2):
-                        j = 2 * k + jj
                         for G in range(2):
+                            lo = G * 512 + (2 * k + jj) * 128
                             nc.tensor.matmul_mx(
                                 out=bank[:, jj * 256 : (jj + 1) * 256],
-                                lhsT=c1[(i, G)][:, j * 128 : (j + 1) * 128].bitcast(FP8X4),
-                                lhsT_scale=s1[(i, G)][:, j * 128 : (j + 1) * 128],
+                                lhsT=c[:, lo : lo + 128].bitcast(FP8X4),
+                                lhsT_scale=s[:, lo : lo + 128],
                                 rhs=ccodes[:, G * 256 : (G + 1) * 256].bitcast(FP8X4),
                                 rhs_scale=cscales[:, G * 256 : (G + 1) * 256],
                                 start=(G == 0),
@@ -264,22 +239,13 @@ def tile_ca3_recurrentmatrix_pa_kernel(tc, current, memory_matrix, out):
 
             def evac1(i):
                 uT = pha.tile([P, 4, 256], F32, name="uT", tag="uT", bufs=2)
-                if i in EV1V:
-                    for k in range(2):
-                        nc.vector.tensor_tensor(
-                            out=uT[:, 2 * k : 2 * k + 2, :],
-                            in0=bD[(i, k)][:].rearrange("p (j b) -> p j b", j=2),
-                            in1=rmn[:, 4 * i + 2 * k : 4 * i + 2 * k + 2].unsqueeze(2).to_broadcast([P, 2, 256]),
-                            op=ALU.mult,
-                        )
-                else:
-                    for j in range(4):
-                        nc.scalar.activation(
-                            out=uT[:, j, :],
-                            in_=bD[(i, j // 2)][:, (j % 2) * 256 : (j % 2 + 1) * 256],
-                            func=ACT.Copy,
-                            scale=rmn[:, 4 * i + j : 4 * i + j + 1],
-                        )
+                for k in range(2):
+                    nc.vector.tensor_tensor(
+                        out=uT[:, 2 * k : 2 * k + 2, :],
+                        in0=bD[(i, k)][:].rearrange("p (j b) -> p j b", j=2),
+                        in1=rmn[:, 4 * i + 2 * k : 4 * i + 2 * k + 2].unsqueeze(2).to_broadcast([P, 2, 256]),
+                        op=ALU.mult,
+                    )
                 uTs[i] = uT
 
             def back(i):
@@ -308,7 +274,7 @@ def tile_ca3_recurrentmatrix_pa_kernel(tc, current, memory_matrix, out):
 
             def cur_path():
                 cur32 = curt[:].bitcast(F32)
-                gcur = pha.tile([P, 2048], BF16, name="gcur", tag="g1", bufs=4, align_bytes=64)
+                gcur = pha.tile([P, 2048], BF16, name="gcur", tag="g1", bufs=2, align_bytes=64)
                 gcur32 = gcur[:].bitcast(F32)
                 for G in range(2):
                     bank = psT.tile([P, 512], F32, name="bankT", tag="T")
@@ -325,34 +291,13 @@ def tile_ca3_recurrentmatrix_pa_kernel(tc, current, memory_matrix, out):
                     )
                 nc.vector.quantize_mx(out=ccodes[:].bitcast(FP8X4), scales=cscales[:], in_=gcur[:])
 
-            def evT(i):
-                evacT(i, "v")
-
-            def evTs(i):
-                evacT(i, "s")
-
-            def rg(i):
-                if 0 < i < d0:
-                    if i not in GREG:
-                        regroup(i, 0, "v")
-                    regroup(i, 1, "v")
-
-            def rgg(i):
-                if i in GREG:
-                    regroup(i, 0, "g")
-
-            def q2(i):
-                if 0 < i < d0:
-                    quant2(i, 1)
-                if 0 < i:
-                    quant2(i, 0)
-
             ops = {
-                "T": transposes, "TA": t_a, "TB": t_b, "evT": evT, "evTs": evTs, "gram": gram, "diag": diag, "sqrtg": sqrtg, "norms": norms,
-                "recip": recip, "q1": quant1, "mm1": mm1, "ev1": evac1, "back": back, "ev2": evac2, "rg": rg, "q2": q2, "rgg": rgg,
+                "T": transposes, "evT": ev_v, "evTs": ev_s, "norms": norms, "recip": recip, "q1": quant1, "mm1": mm1,
+                "ev1": evac1, "back": back, "ev2": evac2, "rg": rg, "q2": q2, "rgg": rgg,
             }
 
             nc.vector.memset(one[:], 1.0)
+            nc.vector.memset(nrm[:], EPS)
             nc.scalar.sqrt(out=one2[:], in_=one[:])
             make_identity(nc, ident_f[:])
             make_identity(nc, ident_b[:])
@@ -362,10 +307,16 @@ def tile_ca3_recurrentmatrix_pa_kernel(tc, current, memory_matrix, out):
             for i in range(1, NB):
                 load(i)
 
-            regroup(0, 0, "v")
-            regroup(0, 1, "v")
-            quant2(0, 0)
-            quant2(0, 1)
+            nlag = [lag for (op, lag) in SCHED if op == "norms"][0]
+            for i in range(-nlag):
+                norms(i)
+            whole(0)
+            vcopy(g2w[0][:], nat[0][:])
+            nc.vector.quantize_mx(
+                out=codes2[:, 0, :].bitcast(FP8X4), scales=scales2[:, 0, :], in_=g2w[0][:].rearrange("p w t -> p (w t)")
+            )
+            q2done.add((0, 0))
+            q2done.add((0, 1))
             last = max(lag for (op, lag) in SCHED)
             for i in range(NCH + last + 1):
                 for op, lag in SCHED if i < NCH else RUNOUT:
@@ -373,12 +324,15 @@ def tile_ca3_recurrentmatrix_pa_kernel(tc, current, memory_matrix, out):
                     if op == "load":
                         if NB <= c:
                             load(c)
-                    elif 0 <= c < NCH:
+                    elif op == "norms":
+                        if -lag <= c < NCH:
+                            norms(c)
+                    elif 0 <= c < NCH and (c > 0 or lag >= 0):
                         ops[op](c)
                 if i == 0:
                     cur_path()
                 if i == d0:
-                    curt2 = both.tile([P, 2, D], BF16, name="curt2", tag="g2", bufs=3, align_bytes=64)
+                    curt2 = both.tile([P, 2, D], BF16, name="curt2", tag="g2h", bufs=2, align_bytes=64)
                     nc.sync.dma_start(out=curt2[:], in_=current.rearrange("(t p) d -> p t d", p=P))
                 if i == NCH:
                     for t in range(2):
@@ -389,8 +343,8 @@ def tile_ca3_recurrentmatrix_pa_kernel(tc, current, memory_matrix, out):
                     nc.gpsimd.tensor_scalar(
                         out=cur02[:], in0=curt2[:], scalar1=0.2, scalar2=0.0, op0=ALU.mult, op1=ALU.add
                     )
-                    for x in range(SREG):
-                        regroup(halves[x][0], halves[x][1], "s")
+                    for i2 in late[:SREG]:
+                        regroup_half(i2, "s")
                 if i >= NCH:
                     some_left(FILL[i - NCH])
             for c in range(NCH + last + 1 + NB, NCH + DEF):
@@ -410,51 +364,43 @@ def tile_ca3_recurrentmatrix_pa_kernel(tc, current, memory_matrix, out):
                 [psD.tile([P, 512], F32, name="acc%d" % h, tag="D") for h in range(2)],
                 [psU.tile([P, 512], F32, name="acc%d" % (2 + h), tag="U") for h in range(2)],
             ]
+            expd = [0]
 
-            def expo(blk):
-                for t in range(2):
-                    e = phb.tile([P, 1024], BF16, name="e", tag="e", bufs=6)
-                    nc.scalar.activation(
-                        out=e[:],
-                        in_=sim[:, t, blk * 1024 : (blk + 1) * 1024],
-                        func=ACT.Exp,
-                        bias=nb[:, t : t + 1],
-                        scale=rcn[:, t : t + 1],
-                        accum_out=rs[:, t, blk : blk + 1],
-                    )
-                    es[(blk, t)] = e
+            def need_exp(g):
+                while expd[0] < len(EXPG) and EXPG[expd[0]][0] <= g:
+                    k = expd[0]
+                    expd[0] += 1
+                    g0, n = EXPG[k]
+                    for t in range(2):
+                        e = phb.tile([P, 1024], BF16, name="e", tag="e", bufs=6)
+                        nc.scalar.activation(
+                            out=e[:, : n * CH],
+                            in_=sim[:, t, g0 * CH : (g0 + n) * CH],
+                            func=ACT.Exp,
+                            bias=nb[:, t : t + 1],
+                            scale=rcn[:, t : t + 1],
+                            accum_out=rs[:, t, k : k + 1],
+                        )
+                        for x in range(n):
+                            es[(g0 + x, t)] = e[:, x * CH : (x + 1) * CH]
 
             def etrans(blk):
                 for gg in range(2):
                     bank = psT.tile([P, 1024], BF16, name="bankE", tag="T")
-                    bv = bank[:].rearrange("p (b t) -> p b t", t=4)
                     for T in range(4):
                         for t in range(2):
-                            if KP:
-                                nc.tensor.matmul(
-                                    out=bv[:, t * 128 : (t + 1) * 128, T],
-                                    lhsT=es[(blk, t)][:, gg * 512 + T * 128 : gg * 512 + (T + 1) * 128],
-                                    rhs=ident_b[:],
-                                    start=True,
-                                    stop=True,
-                                )
-                            else:
-                                nc.tensor.transpose(
-                                    bank[:, T * 256 + t * 128 : T * 256 + (t + 1) * 128],
-                                    es[(blk, t)][:, gg * 512 + T * 128 : gg * 512 + (T + 1) * 128],
-                                    ident_b[:],
-                                )
+                            nc.tensor.transpose(
+                                bank[:, T * 256 + t * 128 : T * 256 + (t + 1) * 128],
+                                es[(2 * blk + gg, t)][:, T * 128 : (T + 1) * 128],
+                                ident_b[:],
+                            )
                     bE[(blk, gg)] = bank
 
             def evac3(blk):
                 ge = phb.tile([P, 2048], BF16, name="ge", tag="ge", bufs=2, align_bytes=64)
                 for gg in range(2):
-                    if KP:
-                        dst = ge[:, gg * 1024 : (gg + 1) * 1024]
-                        src = bE[(blk, gg)][:]
-                    else:
-                        dst = ge[:, gg * 1024 : (gg + 1) * 1024].rearrange("p (b t) -> p b t", t=4)
-                        src = bE[(blk, gg)][:].rearrange("p (t b) -> p b t", t=4)
+                    dst = ge[:, gg * 1024 : (gg + 1) * 1024].rearrange("p (b t) -> p b t", t=4)
+                    src = bE[(blk, gg)][:].rearrange("p (t b) -> p b t", t=4)
                     if gg == 1 and blk in SEV3:
                         nc.scalar.copy(out=dst, in_=src)
                     else:
@@ -484,15 +430,13 @@ def tile_ca3_recurrentmatrix_pa_kernel(tc, current, memory_matrix, out):
                                 stop=(g == NCH - 1),
                             )
 
-            expo(0)
-            expo(1)
+            need_exp(3)
             etrans(0)
             some_left(FILLB[0])
             evac3(0)
             quante(0)
             for blk in range(NBLK):
-                if blk + 2 < NBLK:
-                    expo(blk + 2)
+                need_exp(2 * (blk + 2) + 1)
                 if blk + 1 < NBLK:
                     etrans(blk + 1)
                 while any((g, h) not in q2done for g in (2 * blk, 2 * blk + 1) for h in range(2)):

@@ -42,7 +42,6 @@ def tile_ca3_recurrentmatrix_pa_kernel(tc, current, memory_matrix, out):
         psU = ctx.enter_context(tc.psum_pool(name="psU", bufs=2))
 
         ident_f = keep.tile([P, P], F32, name="ident_f")
-        ident_b = keep.tile([P, P], BF16, name="ident_b")
         codes2 = keep.tile([P, NCH, D], U32, name="codes2", align_bytes=64)
         scales2 = keep.tile([P, NCH, D], U8, name="scales2", align_bytes=64)
         sim = keep.tile([P, 2, C], F32, name="sim")
@@ -263,8 +262,8 @@ def tile_ca3_recurrentmatrix_pa_kernel(tc, current, memory_matrix, out):
             def evac2(i):
                 for t in range(2):
                     nc.vector.tensor_scalar(
-                        out=sim[:, t, i * CH : (i + 1) * CH],
-                        in0=bU[(i, t)][:],
+                        out=sim[:, t, i * CH : (i + 1) * CH].rearrange("p (u n e) -> p u n e", u=2, e=2),
+                        in0=bU[(i, t)][:].rearrange("p (u e n) -> p u n e", u=2, e=2),
                         scalar1=1.0,
                         scalar2=None,
                         op0=ALU.mult,
@@ -300,7 +299,6 @@ def tile_ca3_recurrentmatrix_pa_kernel(tc, current, memory_matrix, out):
             nc.vector.memset(nrm[:], EPS)
             nc.scalar.sqrt(out=one2[:], in_=one[:])
             make_identity(nc, ident_f[:])
-            make_identity(nc, ident_b[:])
             load(0, True)
             curt = pha.tile([P, 2, D], BF16, name="curt", tag="uT", bufs=2)
             nc.sync.dma_start(out=curt[:], in_=current.rearrange("(t p) d -> p t d", p=P))
@@ -386,21 +384,22 @@ def tile_ca3_recurrentmatrix_pa_kernel(tc, current, memory_matrix, out):
 
             def etrans(blk):
                 for gg in range(2):
-                    bank = psT.tile([P, 1024], BF16, name="bankE", tag="T")
-                    for T in range(4):
-                        for t in range(2):
+                    bank = psT.tile([P, 512], F32, name="bankE", tag="T")
+                    for t in range(2):
+                        words = es[(2 * blk + gg, t)].bitcast(F32)
+                        for u in range(2):
                             nc.tensor.transpose(
-                                bank[:, T * 256 + t * 128 : T * 256 + (t + 1) * 128],
-                                es[(2 * blk + gg, t)][:, T * 128 : (T + 1) * 128],
-                                ident_b[:],
+                                bank[:, u * 256 + t * 128 : u * 256 + (t + 1) * 128],
+                                words[:, u * 128 : (u + 1) * 128],
+                                ident_f[:],
                             )
                     bE[(blk, gg)] = bank
 
             def evac3(blk):
                 ge = phb.tile([P, 2048], BF16, name="ge", tag="ge", bufs=2, align_bytes=64)
                 for gg in range(2):
-                    dst = ge[:, gg * 1024 : (gg + 1) * 1024].rearrange("p (b t) -> p b t", t=4)
-                    src = bE[(blk, gg)][:].rearrange("p (t b) -> p b t", t=4)
+                    dst = ge[:].bitcast(F32)[:, gg * 512 : (gg + 1) * 512].rearrange("p (b u) -> p b u", u=2)
+                    src = bE[(blk, gg)][:].rearrange("p (u b) -> p b u", u=2)
                     if gg == 1 and blk in SEV3:
                         nc.scalar.copy(out=dst, in_=src)
                     else:

@@ -20,13 +20,10 @@ CH = 512
 NCH = C // CH
 NBLK = NCH // 2
 NB = 3
-DEF = 9
-SREG = 1
-FILL = [0, 0, 0, 0, 0, 0, 0, 0]
-FILLB = [4, 3, 1, 2, 2, 2, 2, 2]
-SEV3 = [1, 2, 3, 4, 5, 6, 7]
-VEVL = [4, 2, 4, 2, 1, 0, 2, 1, 0, 3, 2, 2, 4, 4, 0, 1]
-EXPG = [(0, 2), (2, 2), (4, 2), (6, 2), (8, 2), (10, 2), (12, 2), (14, 2)]
+DEF = 10
+GREG = 2
+SEV = [5, 2]
+FILLB = [1, 2, 2, 2, 3, 3, 3, 2]
 SCHED = [("T", 0), ("ev2", 3), ("ev1", 2), ("back", 2), ("evTs", 0), ("q1", 1), ("mm1", 1), ("rg", 0), ("q2", 0), ("evT", 0), ("rgg", -1), ("load", -3), ("norms", -1), ("recip", 0)]
 RUNOUT = [("ev1", 2), ("q1", 1), ("mm1", 1), ("ev2", 3), ("back", 2), ("load", -3)]
 
@@ -59,7 +56,7 @@ def tile_ca3_recurrentmatrix_pa_kernel(tc, current, memory_matrix, out):
         mx = keep.tile([P, 2, NCH], F32, name="mx")
         mu = keep.tile([P, 2], F32, name="mu")
         nb = keep.tile([P, 2], F32, name="nb")
-        rs = keep.tile([P, 2, len(EXPG)], F32, name="rs")
+        rs = keep.tile([P, 2, NBLK + 1], F32, name="rs")
         rsum = keep.tile([P, 2], F32, name="rsum")
         rinv = keep.tile([P, 2], F32, name="rinv")
         wgt = keep.tile([P, 2], F32, name="wgt")
@@ -125,6 +122,15 @@ def tile_ca3_recurrentmatrix_pa_kernel(tc, current, memory_matrix, out):
             t = both.tile([P, 512, 4], BF16, name="g2h", tag="g2h", bufs=2, align_bytes=64)
             if eng == "v":
                 vcopy(t[:], nat[i][:, :, 512:])
+            elif eng == "g":
+                nc.gpsimd.tensor_scalar(
+                    out=t[:],
+                    in0=nat[i][:, :, 512:].rearrange("p t w -> p w t"),
+                    scalar1=1.0,
+                    scalar2=0.0,
+                    op0=ALU.mult,
+                    op1=ALU.add,
+                )
             else:
                 nc.scalar.copy(out=t[:], in_=nat[i][:, :, 512:].rearrange("p t w -> p w t"))
             g2h[i] = t
@@ -138,8 +144,8 @@ def tile_ca3_recurrentmatrix_pa_kernel(tc, current, memory_matrix, out):
             )
 
         late = list(range(d0, NCH))
-        left = [("q", i) for i in late[:SREG]]
-        for i in late[SREG:]:
+        left = [("q", i) for i in late[:GREG]]
+        for i in late[GREG:]:
             left += [("r", i), ("q", i)]
         done = [0]
 
@@ -176,12 +182,19 @@ def tile_ca3_recurrentmatrix_pa_kernel(tc, current, memory_matrix, out):
                             )
                     bT[(i, b)] = bank
 
+            def vshare(i):
+                if i == 0:
+                    return 4
+                if i < d0:
+                    return 1
+                return 2 + i % 2
+
             def evac_t(i, eng):
                 if i not in g1:
                     g1[i] = pha.tile([P, 4096], BF16, name="g1", tag="g1", bufs=2, align_bytes=64)
                 g32 = g1[i][:].bitcast(F32)
                 for b in range(4):
-                    on_v = b >= 4 - VEVL[i]
+                    on_v = b >= 4 - vshare(i)
                     if on_v != (eng == "v"):
                         continue
                     dst = g32[:, b * 512 : (b + 1) * 512].rearrange("p (j c u) -> p j c u", j=2, u=2)
@@ -239,6 +252,15 @@ def tile_ca3_recurrentmatrix_pa_kernel(tc, current, memory_matrix, out):
             def evac1(i):
                 uT = pha.tile([P, 4, 256], F32, name="uT", tag="uT", bufs=2)
                 for k in range(2):
+                    if i >= NCH - 2:
+                        for j in range(2 * k, 2 * k + 2):
+                            nc.scalar.activation(
+                                out=uT[:, j, :],
+                                in_=bD[(i, k)][:, (j % 2) * 256 : (j % 2 + 1) * 256],
+                                func=ACT.Copy,
+                                scale=rmn[:, 4 * i + j : 4 * i + j + 1],
+                            )
+                        continue
                     nc.vector.tensor_tensor(
                         out=uT[:, 2 * k : 2 * k + 2, :],
                         in0=bD[(i, k)][:].rearrange("p (j b) -> p j b", j=2),
@@ -308,6 +330,10 @@ def tile_ca3_recurrentmatrix_pa_kernel(tc, current, memory_matrix, out):
             nlag = [lag for (op, lag) in SCHED if op == "norms"][0]
             for i in range(-nlag):
                 norms(i)
+            for t in range(2):
+                nc.scalar.activation(out=junk[:], in_=curt[:, t, :], func=ACT.Square, accum_out=cn2[:, t : t + 1])
+            nc.scalar.sqrt(out=cnrm[:], in_=cn2[:])
+            nc.gpsimd.tensor_scalar(out=cur02[:], in0=curt[:], scalar1=0.2, scalar2=0.0, op0=ALU.mult, op1=ALU.add)
             whole(0)
             vcopy(g2w[0][:], nat[0][:])
             nc.vector.quantize_mx(
@@ -329,22 +355,9 @@ def tile_ca3_recurrentmatrix_pa_kernel(tc, current, memory_matrix, out):
                         ops[op](c)
                 if i == 0:
                     cur_path()
-                if i == d0:
-                    curt2 = both.tile([P, 2, D], BF16, name="curt2", tag="g2h", bufs=2, align_bytes=64)
-                    nc.sync.dma_start(out=curt2[:], in_=current.rearrange("(t p) d -> p t d", p=P))
                 if i == NCH:
-                    for t in range(2):
-                        nc.scalar.activation(
-                            out=junk[:], in_=curt2[:, t, :], func=ACT.Square, accum_out=cn2[:, t : t + 1]
-                        )
-                    nc.scalar.sqrt(out=cnrm[:], in_=cn2[:])
-                    nc.gpsimd.tensor_scalar(
-                        out=cur02[:], in0=curt2[:], scalar1=0.2, scalar2=0.0, op0=ALU.mult, op1=ALU.add
-                    )
-                    for i2 in late[:SREG]:
-                        regroup_half(i2, "s")
-                if i >= NCH:
-                    some_left(FILL[i - NCH])
+                    for i2 in late[:GREG]:
+                        regroup_half(i2, "g")
             for c in range(NCH + last + 1 + NB, NCH + DEF):
                 load(c)
             nc.vector.tensor_scalar_max(out=cnrmc[:], in0=cnrm[:], scalar1=EPS)
@@ -354,6 +367,7 @@ def tile_ca3_recurrentmatrix_pa_kernel(tc, current, memory_matrix, out):
             nc.vector.tensor_reduce(out=mu[:], in_=mx[:], axis=AX.X, op=ALU.max)
             nc.vector.scalar_tensor_tensor(out=nb[:], in0=mu[:], scalar=-1.0, in1=rcn[:], op0=ALU.mult, op1=ALU.mult)
 
+            units = [[0], [1]] + [[2 * k, 2 * k + 1] for k in range(1, NBLK)]
             es = {}
             bE = {}
             ges = {}
@@ -362,66 +376,61 @@ def tile_ca3_recurrentmatrix_pa_kernel(tc, current, memory_matrix, out):
                 [psD.tile([P, 512], F32, name="acc%d" % h, tag="D") for h in range(2)],
                 [psU.tile([P, 512], F32, name="acc%d" % (2 + h), tag="U") for h in range(2)],
             ]
-            expd = [0]
 
-            def need_exp(g):
-                while expd[0] < len(EXPG) and EXPG[expd[0]][0] <= g:
-                    k = expd[0]
-                    expd[0] += 1
-                    g0, n = EXPG[k]
-                    for t in range(2):
-                        e = phb.tile([P, 1024], BF16, name="e", tag="e", bufs=6)
-                        nc.scalar.activation(
-                            out=e[:, : n * CH],
-                            in_=sim[:, t, g0 * CH : (g0 + n) * CH],
-                            func=ACT.Exp,
-                            bias=nb[:, t : t + 1],
-                            scale=rcn[:, t : t + 1],
-                            accum_out=rs[:, t, k : k + 1],
-                        )
-                        for x in range(n):
-                            es[(g0 + x, t)] = e[:, x * CH : (x + 1) * CH]
+            def exps(x):
+                g0, n = units[x][0], len(units[x])
+                for t in range(2):
+                    e = phb.tile([P, 2 * CH], BF16, name="e", tag="e", bufs=6)
+                    nc.scalar.activation(
+                        out=e[:, : n * CH],
+                        in_=sim[:, t, g0 * CH : (g0 + n) * CH],
+                        func=ACT.Exp,
+                        bias=nb[:, t : t + 1],
+                        scale=rcn[:, t : t + 1],
+                        accum_out=rs[:, t, x : x + 1],
+                    )
+                    es[(x, t)] = e
 
-            def etrans(blk):
-                for gg in range(2):
+            def etrans(x):
+                for gg in range(len(units[x])):
                     bank = psT.tile([P, 512], F32, name="bankE", tag="T")
                     for t in range(2):
-                        words = es[(2 * blk + gg, t)].bitcast(F32)
+                        words = es[(x, t)][:].bitcast(F32)
                         for u in range(2):
                             nc.tensor.transpose(
                                 bank[:, u * 256 + t * 128 : u * 256 + (t + 1) * 128],
-                                words[:, u * 128 : (u + 1) * 128],
+                                words[:, gg * 256 + u * 128 : gg * 256 + (u + 1) * 128],
                                 ident_f[:],
                             )
-                    bE[(blk, gg)] = bank
+                    bE[(x, gg)] = bank
 
-            def evac3(blk):
+            def evac3(x):
                 ge = phb.tile([P, 2048], BF16, name="ge", tag="ge", bufs=2, align_bytes=64)
-                for gg in range(2):
+                for gg in range(len(units[x])):
                     dst = ge[:].bitcast(F32)[:, gg * 512 : (gg + 1) * 512].rearrange("p (b u) -> p b u", u=2)
-                    src = bE[(blk, gg)][:].rearrange("p (u b) -> p b u", u=2)
-                    if gg == 1 and blk in SEV3:
+                    src = bE[(x, gg)][:].rearrange("p (u b) -> p b u", u=2)
+                    if x >= SEV[gg]:
                         nc.scalar.copy(out=dst, in_=src)
                     else:
                         nc.vector.tensor_copy(out=dst, in_=src)
-                ges[blk] = ge
+                ges[x] = ge
 
-            def quante(blk):
-                c = phb.tile([P, 512], U32, name="ec", tag="ec", bufs=2, align_bytes=64)
+            def quante(x):
+                w = 256 * len(units[x])
+                cd = phb.tile([P, 512], U32, name="ec", tag="ec", bufs=2, align_bytes=64)
                 s = phb.tile([P, 512], U8, name="esc", tag="esc", bufs=2, align_bytes=64)
-                nc.vector.quantize_mx(out=c[:].bitcast(FP8X4), scales=s[:], in_=ges[blk][:])
-                ecs[blk] = (c, s)
+                nc.vector.quantize_mx(out=cd[:, :w].bitcast(FP8X4), scales=s[:, :w], in_=ges[x][:, : 4 * w])
+                ecs[x] = (cd, s)
 
-            def mm2(blk):
-                c, s = ecs[blk]
+            def mm2(x):
+                cd, s = ecs[x]
                 for t in range(2):
-                    for gg in range(2):
-                        g = 2 * blk + gg
-                        lo = gg * 256 + t * 128
-                        for h in range(2):
+                    for h in range(2):
+                        for gg, g in enumerate(units[x]):
+                            lo = gg * 256 + t * 128
                             nc.tensor.matmul_mx(
                                 out=acc[t][h][:],
-                                lhsT=c[:, lo : lo + 128].bitcast(FP8X4),
+                                lhsT=cd[:, lo : lo + 128].bitcast(FP8X4),
                                 lhsT_scale=s[:, lo : lo + 128],
                                 rhs=codes2[:, g, h * 512 : (h + 1) * 512].bitcast(FP8X4),
                                 rhs_scale=scales2[:, g, h * 512 : (h + 1) * 512],
@@ -429,22 +438,25 @@ def tile_ca3_recurrentmatrix_pa_kernel(tc, current, memory_matrix, out):
                                 stop=(g == NCH - 1),
                             )
 
-            need_exp(3)
+            exps(0)
+            exps(1)
+            exps(2)
             etrans(0)
-            some_left(FILLB[0])
+            some_left(2)
             evac3(0)
             quante(0)
-            for blk in range(NBLK):
-                need_exp(2 * (blk + 2) + 1)
-                if blk + 1 < NBLK:
-                    etrans(blk + 1)
-                while any((g, h) not in q2done for g in (2 * blk, 2 * blk + 1) for h in range(2)):
+            for x in range(len(units)):
+                if x + 1 < len(units):
+                    etrans(x + 1)
+                while any((g, h) not in q2done for g in units[x] for h in range(2)):
                     some_left(1)
-                mm2(blk)
-                if blk + 1 < NBLK:
-                    evac3(blk + 1)
-                    some_left(FILLB[blk + 1])
-                    quante(blk + 1)
+                mm2(x)
+                if x + 1 < len(units):
+                    evac3(x + 1)
+                    quante(x + 1)
+                    if x + 3 < len(units):
+                        exps(x + 3)
+                    some_left(FILLB[x])
             nc.vector.tensor_reduce(out=rsum[:], in_=rs[:], axis=AX.X, op=ALU.add)
             nc.vector.reciprocal(out=rinv[:], in_=rsum[:])
             nc.vector.tensor_scalar_mul(out=wgt[:], in0=rinv[:], scalar1=0.8)

@@ -21,11 +21,10 @@ NCH = C // CH
 NBLK = NCH // 2
 NB = 3
 DEF = 10
-GREG = 2
 SEV = [5, 2]
-FILLB = [1, 2, 2, 2, 3, 3, 3, 2]
-SCHED = [("T", 0), ("ev2", 3), ("ev1", 2), ("back", 2), ("evTs", 0), ("q1", 1), ("mm1", 1), ("rg", 0), ("q2", 0), ("evT", 0), ("rgg", -1), ("load", -3), ("norms", -1), ("recip", 0)]
-RUNOUT = [("ev1", 2), ("q1", 1), ("mm1", 1), ("ev2", 3), ("back", 2), ("load", -3)]
+FILLB = [2, 2, 2, 3, 3, 3, 3, 2]
+SCHED = [("T", 0), ("floor", 1), ("ev2", 3), ("recip", 1), ("ev1", 2), ("back", 2), ("evTs", 0), ("rg", 0), ("q1", 1), ("mm1", 1), ("q2", 0), ("evT", 0), ("rgg", -1), ("load", -3), ("norms", -1)]
+RUNOUT = [("floor", 1), ("recip", 1), ("ev1", 2), ("q1", 1), ("mm1", 1), ("ev2", 3), ("back", 2), ("load", -3)]
 
 
 def tile_ca3_recurrentmatrix_pa_kernel(tc, current, memory_matrix, out):
@@ -43,6 +42,7 @@ def tile_ca3_recurrentmatrix_pa_kernel(tc, current, memory_matrix, out):
         scales2 = keep.tile([P, NCH, D], U8, name="scales2", align_bytes=64)
         sim = keep.tile([P, 2, C], F32, name="sim")
         cur02 = keep.tile([P, 2, D], F32, name="cur02")
+        curt2 = keep.tile([P, 2, D], BF16, name="curt2")
         ccodes = keep.tile([P, 512], U32, name="ccodes", align_bytes=64)
         cscales = keep.tile([P, 512], U8, name="cscales", align_bytes=64)
         n2 = keep.tile([P, 4 * NCH], F32, name="n2")
@@ -122,15 +122,6 @@ def tile_ca3_recurrentmatrix_pa_kernel(tc, current, memory_matrix, out):
             t = both.tile([P, 512, 4], BF16, name="g2h", tag="g2h", bufs=2, align_bytes=64)
             if eng == "v":
                 vcopy(t[:], nat[i][:, :, 512:])
-            elif eng == "g":
-                nc.gpsimd.tensor_scalar(
-                    out=t[:],
-                    in0=nat[i][:, :, 512:].rearrange("p t w -> p w t"),
-                    scalar1=1.0,
-                    scalar2=0.0,
-                    op0=ALU.mult,
-                    op1=ALU.add,
-                )
             else:
                 nc.scalar.copy(out=t[:], in_=nat[i][:, :, 512:].rearrange("p t w -> p w t"))
             g2h[i] = t
@@ -144,8 +135,8 @@ def tile_ca3_recurrentmatrix_pa_kernel(tc, current, memory_matrix, out):
             )
 
         late = list(range(d0, NCH))
-        left = [("q", i) for i in late[:GREG]]
-        for i in late[GREG:]:
+        left = []
+        for i in late:
             left += [("r", i), ("q", i)]
         done = [0]
 
@@ -166,7 +157,7 @@ def tile_ca3_recurrentmatrix_pa_kernel(tc, current, memory_matrix, out):
             bD = {}
             bU = {}
             uTs = {}
-            junk = pha.tile([P, D], BF16, name="junk", bufs=1)
+            junk = [sim[:, :, (NCH - 1 - n) * CH : (NCH - n) * CH] for n in range(3)]
 
             def transposes(i):
                 nat32 = nat[i][:].bitcast(F32)
@@ -213,16 +204,19 @@ def tile_ca3_recurrentmatrix_pa_kernel(tc, current, memory_matrix, out):
             def norms(i):
                 for j in range(4):
                     nc.scalar.activation(
-                        out=junk[:], in_=nat[i][:, j, :], func=ACT.Square, accum_out=n2[:, 4 * i + j : 4 * i + j + 1]
+                        out=junk[j % 3], in_=nat[i][:, j, :].rearrange("p (t w) -> p t w", t=2), func=ACT.Square, accum_out=n2[:, 4 * i + j : 4 * i + j + 1]
                     )
                 if i % 2:
                     nc.scalar.sqrt(out=nrm[:, 4 * i - 4 : 4 * i + 4, 0], in_=n2[:, 4 * i - 4 : 4 * i + 4])
 
-            def recip(i):
+            def floor(i):
                 if i % 2:
                     nc.vector.tensor_reduce(
                         out=nrmc[:, 4 * i - 4 : 4 * i + 4], in_=nrm[:, 4 * i - 4 : 4 * i + 4, :], axis=AX.X, op=ALU.max
                     )
+
+            def recip(i):
+                if i % 2:
                     nc.vector.reciprocal(out=rmn[:, 4 * i - 4 : 4 * i + 4], in_=nrmc[:, 4 * i - 4 : 4 * i + 4])
 
             def quant1(i):
@@ -313,7 +307,7 @@ def tile_ca3_recurrentmatrix_pa_kernel(tc, current, memory_matrix, out):
                 nc.vector.quantize_mx(out=ccodes[:].bitcast(FP8X4), scales=cscales[:], in_=gcur[:])
 
             ops = {
-                "T": transposes, "evT": ev_v, "evTs": ev_s, "norms": norms, "recip": recip, "q1": quant1, "mm1": mm1,
+                "T": transposes, "evT": ev_v, "evTs": ev_s, "norms": norms, "recip": recip, "floor": floor, "q1": quant1, "mm1": mm1,
                 "ev1": evac1, "back": back, "ev2": evac2, "rg": rg, "q2": q2, "rgg": rgg,
             }
 
@@ -330,10 +324,6 @@ def tile_ca3_recurrentmatrix_pa_kernel(tc, current, memory_matrix, out):
             nlag = [lag for (op, lag) in SCHED if op == "norms"][0]
             for i in range(-nlag):
                 norms(i)
-            for t in range(2):
-                nc.scalar.activation(out=junk[:], in_=curt[:, t, :], func=ACT.Square, accum_out=cn2[:, t : t + 1])
-            nc.scalar.sqrt(out=cnrm[:], in_=cn2[:])
-            nc.gpsimd.tensor_scalar(out=cur02[:], in0=curt[:], scalar1=0.2, scalar2=0.0, op0=ALU.mult, op1=ALU.add)
             whole(0)
             vcopy(g2w[0][:], nat[0][:])
             nc.vector.quantize_mx(
@@ -343,6 +333,13 @@ def tile_ca3_recurrentmatrix_pa_kernel(tc, current, memory_matrix, out):
             q2done.add((0, 1))
             last = max(lag for (op, lag) in SCHED)
             for i in range(NCH + last + 1):
+                if i == NCH:
+                    junkc = pha.tile([P, 2, D], BF16, name="junkc", tag="g1", bufs=2, align_bytes=64)
+                    for t in range(2):
+                        nc.scalar.activation(
+                            out=junkc[:, t, :], in_=curt2[:, t, :], func=ACT.Square, accum_out=cn2[:, t : t + 1]
+                        )
+                    nc.scalar.sqrt(out=cnrm[:], in_=cn2[:])
                 for op, lag in SCHED if i < NCH else RUNOUT:
                     c = i - lag
                     if op == "load":
@@ -355,9 +352,8 @@ def tile_ca3_recurrentmatrix_pa_kernel(tc, current, memory_matrix, out):
                         ops[op](c)
                 if i == 0:
                     cur_path()
-                if i == NCH:
-                    for i2 in late[:GREG]:
-                        regroup_half(i2, "g")
+                if i == d0:
+                    nc.sync.dma_start(out=curt2[:], in_=current.rearrange("(t p) d -> p t d", p=P))
             for c in range(NCH + last + 1 + NB, NCH + DEF):
                 load(c)
             nc.vector.tensor_scalar_max(out=cnrmc[:], in0=cnrm[:], scalar1=EPS)
@@ -456,6 +452,8 @@ def tile_ca3_recurrentmatrix_pa_kernel(tc, current, memory_matrix, out):
                     quante(x + 1)
                     if x + 3 < len(units):
                         exps(x + 3)
+                    if x + 3 == len(units):
+                        nc.scalar.activation(out=cur02[:], in_=curt2[:], func=ACT.Copy, scale=0.2)
                     some_left(FILLB[x])
             nc.vector.tensor_reduce(out=rsum[:], in_=rs[:], axis=AX.X, op=ALU.add)
             nc.vector.reciprocal(out=rinv[:], in_=rsum[:])

@@ -22,8 +22,9 @@ NBLK = NCH // 2
 NB = 3
 DEF = 10
 SEV = [5, 2]
+AHEAD = 3
 FILLB = [2, 2, 2, 3, 3, 3, 3, 2]
-SCHED = [("T", 0), ("floor", 1), ("ev2", 3), ("recip", 1), ("ev1", 2), ("back", 2), ("evTs", 0), ("rg", 0), ("q1", 1), ("mm1", 1), ("q2", 0), ("evT", 0), ("rgg", -1), ("load", -3), ("norms", -1)]
+SCHED = [("T", 0), ("floor", 1), ("ev2a", 3), ("recip", 1), ("ev2b", 3), ("ev1", 2), ("back", 2), ("evTs", 0), ("roots", 0), ("rg", 0), ("q1", 1), ("mm1", 1), ("q2", 0), ("evT", 0), ("rgg", -1), ("load", -3), ("norms", -1)]
 RUNOUT = [("floor", 1), ("recip", 1), ("ev1", 2), ("q1", 1), ("mm1", 1), ("ev2", 3), ("back", 2), ("load", -3)]
 
 
@@ -119,9 +120,18 @@ def tile_ca3_recurrentmatrix_pa_kernel(tc, current, memory_matrix, out):
                 q2done.add((i, 1))
 
         def regroup_half(i, eng):
-            t = both.tile([P, 512, 4], BF16, name="g2h", tag="g2h", bufs=2, align_bytes=64)
+            t = both.tile([P, 512, 4], BF16, name="g2h", tag="g2h", bufs=3, align_bytes=64)
             if eng == "v":
                 vcopy(t[:], nat[i][:, :, 512:])
+            elif eng == "g":
+                nc.gpsimd.tensor_scalar(
+                    out=t[:],
+                    in0=nat[i][:, :, 512:].rearrange("p t w -> p w t"),
+                    scalar1=1.0,
+                    scalar2=0.0,
+                    op0=ALU.mult,
+                    op1=ALU.add,
+                )
             else:
                 nc.scalar.copy(out=t[:], in_=nat[i][:, :, 512:].rearrange("p t w -> p w t"))
             g2h[i] = t
@@ -135,10 +145,15 @@ def tile_ca3_recurrentmatrix_pa_kernel(tc, current, memory_matrix, out):
             )
 
         late = list(range(d0, NCH))
-        left = []
-        for i in late:
-            left += [("r", i), ("q", i)]
+        left = [("r", i) for i in late[:AHEAD]]
+        for n, i in enumerate(late):
+            left += [("q", i)]
+            if n + AHEAD < len(late):
+                left += [("r", late[n + AHEAD])]
         done = [0]
+
+        def late_engine(n):
+            return "v"
 
         def some_left(n):
             for x in range(n):
@@ -146,7 +161,7 @@ def tile_ca3_recurrentmatrix_pa_kernel(tc, current, memory_matrix, out):
                     kind, i = left[done[0]]
                     done[0] += 1
                     if kind == "r":
-                        regroup_half(i, "v")
+                        regroup_half(i, late_engine(i - d0))
                     else:
                         quant_half(i)
 
@@ -157,7 +172,7 @@ def tile_ca3_recurrentmatrix_pa_kernel(tc, current, memory_matrix, out):
             bD = {}
             bU = {}
             uTs = {}
-            junk = [sim[:, :, (NCH - 1 - n) * CH : (NCH - n) * CH] for n in range(3)]
+            junk = [sim[:, 1, C - D :], sim[:, 1, C - 2 * D : C - D], sim[:, 0, C - D :]]
 
             def transposes(i):
                 nat32 = nat[i][:].bitcast(F32)
@@ -174,11 +189,7 @@ def tile_ca3_recurrentmatrix_pa_kernel(tc, current, memory_matrix, out):
                     bT[(i, b)] = bank
 
             def vshare(i):
-                if i == 0:
-                    return 4
-                if i < d0:
-                    return 1
-                return 2 + i % 2
+                return 4 if i == 0 else 1 if i < d0 else 2 if i > 12 else 2 + i % 2
 
             def evac_t(i, eng):
                 if i not in g1:
@@ -204,8 +215,10 @@ def tile_ca3_recurrentmatrix_pa_kernel(tc, current, memory_matrix, out):
             def norms(i):
                 for j in range(4):
                     nc.scalar.activation(
-                        out=junk[j % 3], in_=nat[i][:, j, :].rearrange("p (t w) -> p t w", t=2), func=ACT.Square, accum_out=n2[:, 4 * i + j : 4 * i + j + 1]
+                        out=junk[j % 3], in_=nat[i][:, j, :], func=ACT.Square, accum_out=n2[:, 4 * i + j : 4 * i + j + 1]
                     )
+
+            def roots(i):
                 if i % 2:
                     nc.scalar.sqrt(out=nrm[:, 4 * i - 4 : 4 * i + 4, 0], in_=n2[:, 4 * i - 4 : 4 * i + 4])
 
@@ -275,8 +288,14 @@ def tile_ca3_recurrentmatrix_pa_kernel(tc, current, memory_matrix, out):
                         )
                     bU[(i, t)] = bank
 
-            def evac2(i):
-                for t in range(2):
+            def evac2_first(i):
+                evac2(i, (0,))
+
+            def evac2_second(i):
+                evac2(i, (1,))
+
+            def evac2(i, halves=(0, 1)):
+                for t in halves:
                     nc.vector.tensor_scalar(
                         out=sim[:, t, i * CH : (i + 1) * CH].rearrange("p (u n e) -> p u n e", u=2, e=2),
                         in0=bU[(i, t)][:].rearrange("p (u e n) -> p u n e", u=2, e=2),
@@ -307,8 +326,8 @@ def tile_ca3_recurrentmatrix_pa_kernel(tc, current, memory_matrix, out):
                 nc.vector.quantize_mx(out=ccodes[:].bitcast(FP8X4), scales=cscales[:], in_=gcur[:])
 
             ops = {
-                "T": transposes, "evT": ev_v, "evTs": ev_s, "norms": norms, "recip": recip, "floor": floor, "q1": quant1, "mm1": mm1,
-                "ev1": evac1, "back": back, "ev2": evac2, "rg": rg, "q2": q2, "rgg": rgg,
+                "T": transposes, "evT": ev_v, "evTs": ev_s, "norms": norms, "recip": recip, "floor": floor, "roots": roots, "q1": quant1, "mm1": mm1,
+                "ev1": evac1, "back": back, "ev2": evac2, "ev2a": evac2_first, "ev2b": evac2_second, "rg": rg, "q2": q2, "rgg": rgg,
             }
 
             nc.vector.memset(one[:], 1.0)
@@ -352,12 +371,16 @@ def tile_ca3_recurrentmatrix_pa_kernel(tc, current, memory_matrix, out):
                         ops[op](c)
                 if i == 0:
                     cur_path()
+                if i == NCH + 1:
+                    nc.scalar.activation(out=cur02[:], in_=curt2[:], func=ACT.Copy, scale=0.2)
+                if i == NCH:
+                    nc.vector.tensor_scalar_max(out=cnrmc[:], in0=cnrm[:], scalar1=EPS)
+                if i == NCH + 1:
+                    nc.vector.reciprocal(out=rcn[:], in_=cnrmc[:])
                 if i == d0:
                     nc.sync.dma_start(out=curt2[:], in_=current.rearrange("(t p) d -> p t d", p=P))
             for c in range(NCH + last + 1 + NB, NCH + DEF):
                 load(c)
-            nc.vector.tensor_scalar_max(out=cnrmc[:], in0=cnrm[:], scalar1=EPS)
-            nc.vector.reciprocal(out=rcn[:], in_=cnrmc[:])
 
         with tc.tile_pool(name="phb", bufs=2) as phb:
             nc.vector.tensor_reduce(out=mu[:], in_=mx[:], axis=AX.X, op=ALU.max)
@@ -452,8 +475,6 @@ def tile_ca3_recurrentmatrix_pa_kernel(tc, current, memory_matrix, out):
                     quante(x + 1)
                     if x + 3 < len(units):
                         exps(x + 3)
-                    if x + 3 == len(units):
-                        nc.scalar.activation(out=cur02[:], in_=curt2[:], func=ACT.Copy, scale=0.2)
                     some_left(FILLB[x])
             nc.vector.tensor_reduce(out=rsum[:], in_=rs[:], axis=AX.X, op=ALU.add)
             nc.vector.reciprocal(out=rinv[:], in_=rsum[:])

@@ -21,7 +21,7 @@ NCH = C // CH
 NBLK = NCH // 2
 NB = 3
 DEF = 10
-SEV = [5, 2]
+SEV = [4, 2]
 AHEAD = 3
 FILLB = [2, 2, 2, 3, 3, 3, 3, 2]
 SCHED = [("T", 0), ("floor", 1), ("ev2a", 3), ("recip", 1), ("ev2b", 3), ("ev1", 2), ("back", 2), ("evTs", 0), ("roots", 0), ("rg", 0), ("q1", 1), ("mm1", 1), ("q2", 0), ("evT", 0), ("rgg", -1), ("load", -3), ("norms", -1)]
@@ -172,7 +172,7 @@ def tile_ca3_recurrentmatrix_pa_kernel(tc, current, memory_matrix, out):
             bD = {}
             bU = {}
             uTs = {}
-            junk = [sim[:, 1, C - D :], sim[:, 1, C - 2 * D : C - D], sim[:, 0, C - D :]]
+            junk = [sim[:, n % 2, (NCH - 1 - n // 2) * CH : (NCH - n // 2) * CH].bitcast(BF16) for n in range(4)]
 
             def transposes(i):
                 nat32 = nat[i][:].bitcast(F32)
@@ -189,7 +189,7 @@ def tile_ca3_recurrentmatrix_pa_kernel(tc, current, memory_matrix, out):
                     bT[(i, b)] = bank
 
             def vshare(i):
-                return 4 if i == 0 else 1 if i < d0 else 2 if i > 12 else 2 + i % 2
+                return 4 if i == 0 else 1 if i < d0 else 2
 
             def evac_t(i, eng):
                 if i not in g1:
@@ -215,7 +215,7 @@ def tile_ca3_recurrentmatrix_pa_kernel(tc, current, memory_matrix, out):
             def norms(i):
                 for j in range(4):
                     nc.scalar.activation(
-                        out=junk[j % 3], in_=nat[i][:, j, :], func=ACT.Square, accum_out=n2[:, 4 * i + j : 4 * i + j + 1]
+                        out=junk[j], in_=nat[i][:, j, :], func=ACT.Square, accum_out=n2[:, 4 * i + j : 4 * i + j + 1]
                     )
 
             def roots(i):
@@ -308,7 +308,7 @@ def tile_ca3_recurrentmatrix_pa_kernel(tc, current, memory_matrix, out):
 
             def cur_path():
                 cur32 = curt[:].bitcast(F32)
-                gcur = pha.tile([P, 2048], BF16, name="gcur", tag="g1", bufs=2, align_bytes=64)
+                gcur = pha.tile([P, 2048], BF16, name="gcur", tag="c1", bufs=1, align_bytes=64)
                 gcur32 = gcur[:].bitcast(F32)
                 for G in range(2):
                     bank = psT.tile([P, 512], F32, name="bankT", tag="T")
@@ -371,6 +371,8 @@ def tile_ca3_recurrentmatrix_pa_kernel(tc, current, memory_matrix, out):
                         ops[op](c)
                 if i == 0:
                     cur_path()
+                if i == NCH:
+                    nc.scalar.activation(out=one2[:], in_=one[:], func=ACT.Exp)
                 if i == NCH + 1:
                     nc.scalar.activation(out=cur02[:], in_=curt2[:], func=ACT.Copy, scale=0.2)
                 if i == NCH:

@@ -23,9 +23,9 @@ NB = 3
 DEF = 10
 SEV = [4, 2]
 AHEAD = 3
-FILLB = [2, 2, 2, 3, 3, 3, 3, 2]
+FILLB = [2, 2, 2, 3, 3, 2, 2, 2]
 SCHED = [("T", 0), ("floor", 1), ("ev2a", 3), ("recip", 1), ("ev2b", 3), ("ev1", 2), ("back", 2), ("evTs", 0), ("roots", 0), ("rg", 0), ("q1", 1), ("mm1", 1), ("q2", 0), ("evT", 0), ("rgg", -1), ("load", -3), ("norms", -1)]
-RUNOUT = [("floor", 1), ("recip", 1), ("ev1", 2), ("q1", 1), ("mm1", 1), ("ev2", 3), ("back", 2), ("load", -3)]
+RUNOUT = [("floor", 1), ("q1", 1), ("mm1", 1), ("recip", 1), ("ev1", 2), ("back", 2), ("ev2", 3), ("load", -3)]
 
 
 def tile_ca3_recurrentmatrix_pa_kernel(tc, current, memory_matrix, out):
@@ -54,6 +54,7 @@ def tile_ca3_recurrentmatrix_pa_kernel(tc, current, memory_matrix, out):
         cnrm = keep.tile([P, 2], F32, name="cnrm")
         cnrmc = keep.tile([P, 2], F32, name="cnrmc")
         rcn = keep.tile([P, 2], F32, name="rcn")
+        nrcn = keep.tile([P, 2], F32, name="nrcn")
         mx = keep.tile([P, 2, NCH], F32, name="mx")
         mu = keep.tile([P, 2], F32, name="mu")
         nb = keep.tile([P, 2], F32, name="nb")
@@ -241,7 +242,10 @@ def tile_ca3_recurrentmatrix_pa_kernel(tc, current, memory_matrix, out):
             def mm1(i):
                 c, s = c1[i]
                 for k in range(2):
-                    bank = psD.tile([P, 512], F32, name="bankD", tag="D")
+                    if i == NCH - 1:
+                        bank = psT.tile([P, 512], F32, name="bankD2", tag="T")
+                    else:
+                        bank = psD.tile([P, 512], F32, name="bankD", tag="D")
                     for jj in range(2):
                         for G in range(2):
                             lo = G * 512 + (2 * k + jj) * 128
@@ -259,7 +263,7 @@ def tile_ca3_recurrentmatrix_pa_kernel(tc, current, memory_matrix, out):
             def evac1(i):
                 uT = pha.tile([P, 4, 256], F32, name="uT", tag="uT", bufs=2)
                 for k in range(2):
-                    if i >= NCH - 2:
+                    if i >= NCH - 1:
                         for j in range(2 * k, 2 * k + 2):
                             nc.scalar.activation(
                                 out=uT[:, j, :],
@@ -305,6 +309,15 @@ def tile_ca3_recurrentmatrix_pa_kernel(tc, current, memory_matrix, out):
                         op1=ALU.max,
                         accum_out=mx[:, t, i : i + 1],
                     )
+                    if i == NCH - 1:
+                        nc.vector.scalar_tensor_tensor(
+                            out=nb[:, t : t + 1],
+                            in0=mx[:, t, i : i + 1],
+                            scalar=mu[:, t : t + 1],
+                            in1=nrcn[:, t : t + 1],
+                            op0=ALU.max,
+                            op1=ALU.mult,
+                        )
 
             def cur_path():
                 cur32 = curt[:].bitcast(F32)
@@ -377,16 +390,17 @@ def tile_ca3_recurrentmatrix_pa_kernel(tc, current, memory_matrix, out):
                     nc.scalar.activation(out=cur02[:], in_=curt2[:], func=ACT.Copy, scale=0.2)
                 if i == NCH:
                     nc.vector.tensor_scalar_max(out=cnrmc[:], in0=cnrm[:], scalar1=EPS)
-                if i == NCH + 1:
+                if i == NCH:
                     nc.vector.reciprocal(out=rcn[:], in_=cnrmc[:])
+                if i == NCH + 1:
+                    nc.vector.tensor_scalar_mul(out=nrcn[:], in0=rcn[:], scalar1=-1.0)
+                    nc.vector.tensor_reduce(out=mu[:], in_=mx[:, :, : NCH - 1], axis=AX.X, op=ALU.max)
                 if i == d0:
                     nc.sync.dma_start(out=curt2[:], in_=current.rearrange("(t p) d -> p t d", p=P))
             for c in range(NCH + last + 1 + NB, NCH + DEF):
                 load(c)
 
         with tc.tile_pool(name="phb", bufs=2) as phb:
-            nc.vector.tensor_reduce(out=mu[:], in_=mx[:], axis=AX.X, op=ALU.max)
-            nc.vector.scalar_tensor_tensor(out=nb[:], in0=mu[:], scalar=-1.0, in1=rcn[:], op0=ALU.mult, op1=ALU.mult)
 
             units = [[0], [1]] + [[2 * k, 2 * k + 1] for k in range(1, NBLK)]
             es = {}
@@ -443,21 +457,20 @@ def tile_ca3_recurrentmatrix_pa_kernel(tc, current, memory_matrix, out):
                 nc.vector.quantize_mx(out=cd[:, :w].bitcast(FP8X4), scales=s[:, :w], in_=ges[x][:, : 4 * w])
                 ecs[x] = (cd, s)
 
-            def mm2(x):
+            def mm2(x, h):
                 cd, s = ecs[x]
                 for t in range(2):
-                    for h in range(2):
-                        for gg, g in enumerate(units[x]):
-                            lo = gg * 256 + t * 128
-                            nc.tensor.matmul_mx(
-                                out=acc[t][h][:],
-                                lhsT=cd[:, lo : lo + 128].bitcast(FP8X4),
-                                lhsT_scale=s[:, lo : lo + 128],
-                                rhs=codes2[:, g, h * 512 : (h + 1) * 512].bitcast(FP8X4),
-                                rhs_scale=scales2[:, g, h * 512 : (h + 1) * 512],
-                                start=(g == 0),
-                                stop=(g == NCH - 1),
-                            )
+                    for gg, g in enumerate(units[x]):
+                        lo = gg * 256 + t * 128
+                        nc.tensor.matmul_mx(
+                            out=acc[t][h][:],
+                            lhsT=cd[:, lo : lo + 128].bitcast(FP8X4),
+                            lhsT_scale=s[:, lo : lo + 128],
+                            rhs=codes2[:, g, h * 512 : (h + 1) * 512].bitcast(FP8X4),
+                            rhs_scale=scales2[:, g, h * 512 : (h + 1) * 512],
+                            start=(g == 0),
+                            stop=(g == NCH - 1),
+                        )
 
             exps(0)
             exps(1)
@@ -469,20 +482,24 @@ def tile_ca3_recurrentmatrix_pa_kernel(tc, current, memory_matrix, out):
             for x in range(len(units)):
                 if x + 1 < len(units):
                     etrans(x + 1)
-                while any((g, h) not in q2done for g in units[x] for h in range(2)):
-                    some_left(1)
-                mm2(x)
+                for h in range(2):
+                    while any((g, h) not in q2done for g in units[x]):
+                        some_left(1)
+                    mm2(x, h)
                 if x + 1 < len(units):
                     evac3(x + 1)
                     quante(x + 1)
                     if x + 3 < len(units):
                         exps(x + 3)
+                    if x + 2 == len(units):
+                        nc.vector.tensor_reduce(out=rsum[:], in_=rs[:], axis=AX.X, op=ALU.add)
+                        some_left(1)
+                        nc.vector.reciprocal(out=rinv[:], in_=rsum[:])
+                        some_left(1)
+                        nc.vector.tensor_scalar_mul(out=wgt[:], in0=rinv[:], scalar1=0.8)
                     some_left(FILLB[x])
-            nc.vector.tensor_reduce(out=rsum[:], in_=rs[:], axis=AX.X, op=ALU.add)
-            nc.vector.reciprocal(out=rinv[:], in_=rsum[:])
-            nc.vector.tensor_scalar_mul(out=wgt[:], in0=rinv[:], scalar1=0.8)
-            for t in range(2):
-                for h in range(2):
+            for h in range(2):
+                for t in range(2):
                     o = phb.tile([P, 512], F32, name="o", tag="o", bufs=4)
                     nc.vector.scalar_tensor_tensor(
                         out=o[:],

@@ -20,12 +20,12 @@ CH = 512
 NCH = C // CH
 NBLK = NCH // 2
 NB = 3
-DEF = 10
-SEV = [4, 2]
+DEF = 12
+SEV = [2, 2]
 AHEAD = 3
-FILLB = [2, 2, 2, 3, 3, 2, 2, 2]
-SCHED = [("T", 0), ("floor", 1), ("ev2a", 3), ("recip", 1), ("ev2b", 3), ("ev1", 2), ("back", 2), ("evTs", 0), ("roots", 0), ("rg", 0), ("q1", 1), ("mm1", 1), ("q2", 0), ("evT", 0), ("rgg", -1), ("load", -3), ("norms", -1)]
-RUNOUT = [("floor", 1), ("q1", 1), ("mm1", 1), ("recip", 1), ("ev1", 2), ("back", 2), ("ev2", 3), ("load", -3)]
+FILLB = [3, 3, 3, 3, 3, 2, 2, 2]
+SCHED = [("T", 0), ("gram", 1), ("ev2a", 3), ("recip", 2), ("ev2b", 3), ("ev1", 2), ("back", 2), ("evTs", 0), ("rg", 0), ("q1", 1), ("mm1", 1), ("gx", 1), ("q2", 0), ("evT", 0), ("rgg", -1), ("load", -3), ("norms", -1), ("roots", 1), ("norms2", -1), ("floor", 1)]
+RUNOUT = [("gram", 1), ("gx", 1), ("roots", 1), ("q1", 1), ("mm1", 1), ("recip", 2), ("ev1", 2), ("floor", 1), ("back", 2), ("ev2", 3), ("load", -3)]
 
 
 def tile_ca3_recurrentmatrix_pa_kernel(tc, current, memory_matrix, out):
@@ -168,6 +168,8 @@ def tile_ca3_recurrentmatrix_pa_kernel(tc, current, memory_matrix, out):
 
         with tc.tile_pool(name="pha", bufs=2) as pha:
             g1 = {}
+            bG = {}
+            junkv = pha.tile([P, P], F32, name="junkv", bufs=1)
             c1 = {}
             bT = {}
             bD = {}
@@ -190,7 +192,7 @@ def tile_ca3_recurrentmatrix_pa_kernel(tc, current, memory_matrix, out):
                     bT[(i, b)] = bank
 
             def vshare(i):
-                return 4 if i == 0 else 1 if i < d0 else 2
+                return 4 if i == 0 else 0 if i < d0 else 1
 
             def evac_t(i, eng):
                 if i not in g1:
@@ -213,25 +215,54 @@ def tile_ca3_recurrentmatrix_pa_kernel(tc, current, memory_matrix, out):
             def ev_s(i):
                 evac_t(i, "s")
 
-            def norms(i):
-                for j in range(4):
+            def ngram(i):
+                return 1 if i < 15 else 0
+
+            def gram(i):
+                if ngram(i) == 0:
+                    return
+                bank = psT.tile([P, 512], F32, name="bankG", tag="T")
+                for n in range(ngram(i)):
+                    k, jj = (3 - n) // 2, (3 - n) % 2
+                    for x in range(8):
+                        lo = ((x // 4 * 2 + k) * 2 + jj) * 512
+                        a = g1[i][:, lo + x % 4 : lo + 512 : 4]
+                        nc.tensor.matmul(bank[:, n * 128 : (n + 1) * 128], a, a, start=(x == 0), stop=(x == 7))
+                bG[i] = bank
+
+            def gram_diag(i):
+                for n in range(ngram(i)):
+                    j = 3 - n
+                    nc.vector.scalar_tensor_tensor(
+                        out=junkv[:],
+                        in0=bG[i][:, n * 128 : (n + 1) * 128],
+                        scalar=1.0,
+                        in1=ident_f[:],
+                        op0=ALU.mult,
+                        op1=ALU.mult,
+                        accum_out=n2[:, 4 * i + j : 4 * i + j + 1],
+                    )
+
+            def norms_last(i):
+                norms(i, True)
+
+            def norms(i, last=False):
+                m = 4 - ngram(i)
+                for j in range(m - 1, m) if last else range(m - 1):
                     nc.scalar.activation(
                         out=junk[j], in_=nat[i][:, j, :], func=ACT.Square, accum_out=n2[:, 4 * i + j : 4 * i + j + 1]
                     )
 
             def roots(i):
-                if i % 2:
-                    nc.scalar.sqrt(out=nrm[:, 4 * i - 4 : 4 * i + 4, 0], in_=n2[:, 4 * i - 4 : 4 * i + 4])
+                nc.scalar.sqrt(out=nrm[:, 4 * i : 4 * i + 4, 0], in_=n2[:, 4 * i : 4 * i + 4])
 
             def floor(i):
-                if i % 2:
-                    nc.vector.tensor_reduce(
-                        out=nrmc[:, 4 * i - 4 : 4 * i + 4], in_=nrm[:, 4 * i - 4 : 4 * i + 4, :], axis=AX.X, op=ALU.max
-                    )
+                nc.vector.tensor_reduce(
+                    out=nrmc[:, 4 * i : 4 * i + 4], in_=nrm[:, 4 * i : 4 * i + 4, :], axis=AX.X, op=ALU.max
+                )
 
             def recip(i):
-                if i % 2:
-                    nc.vector.reciprocal(out=rmn[:, 4 * i - 4 : 4 * i + 4], in_=nrmc[:, 4 * i - 4 : 4 * i + 4])
+                nc.vector.reciprocal(out=rmn[:, 4 * i : 4 * i + 4], in_=nrmc[:, 4 * i : 4 * i + 4])
 
             def quant1(i):
                 c = pha.tile([P, 1024], U32, name="c1", tag="c1", bufs=1, align_bytes=64)
@@ -309,15 +340,6 @@ def tile_ca3_recurrentmatrix_pa_kernel(tc, current, memory_matrix, out):
                         op1=ALU.max,
                         accum_out=mx[:, t, i : i + 1],
                     )
-                    if i == NCH - 1:
-                        nc.vector.scalar_tensor_tensor(
-                            out=nb[:, t : t + 1],
-                            in0=mx[:, t, i : i + 1],
-                            scalar=mu[:, t : t + 1],
-                            in1=nrcn[:, t : t + 1],
-                            op0=ALU.max,
-                            op1=ALU.mult,
-                        )
 
             def cur_path():
                 cur32 = curt[:].bitcast(F32)
@@ -339,7 +361,7 @@ def tile_ca3_recurrentmatrix_pa_kernel(tc, current, memory_matrix, out):
                 nc.vector.quantize_mx(out=ccodes[:].bitcast(FP8X4), scales=cscales[:], in_=gcur[:])
 
             ops = {
-                "T": transposes, "evT": ev_v, "evTs": ev_s, "norms": norms, "recip": recip, "floor": floor, "roots": roots, "q1": quant1, "mm1": mm1,
+                "T": transposes, "evT": ev_v, "evTs": ev_s, "norms": norms, "recip": recip, "floor": floor, "gram": gram, "gx": gram_diag, "roots": roots, "norms2": norms_last, "q1": quant1, "mm1": mm1,
                 "ev1": evac1, "back": back, "ev2": evac2, "ev2a": evac2_first, "ev2b": evac2_second, "rg": rg, "q2": q2, "rgg": rgg,
             }
 
@@ -356,6 +378,7 @@ def tile_ca3_recurrentmatrix_pa_kernel(tc, current, memory_matrix, out):
             nlag = [lag for (op, lag) in SCHED if op == "norms"][0]
             for i in range(-nlag):
                 norms(i)
+                norms_last(i)
             whole(0)
             vcopy(g2w[0][:], nat[0][:])
             nc.vector.quantize_mx(
@@ -377,9 +400,9 @@ def tile_ca3_recurrentmatrix_pa_kernel(tc, current, memory_matrix, out):
                     if op == "load":
                         if NB <= c:
                             load(c)
-                    elif op == "norms":
+                    elif op in ("norms", "norms2"):
                         if -lag <= c < NCH:
-                            norms(c)
+                            ops[op](c)
                     elif 0 <= c < NCH and (c > 0 or lag >= 0):
                         ops[op](c)
                 if i == 0:
@@ -401,6 +424,15 @@ def tile_ca3_recurrentmatrix_pa_kernel(tc, current, memory_matrix, out):
                 load(c)
 
         with tc.tile_pool(name="phb", bufs=2) as phb:
+            for t in range(2):
+                nc.vector.scalar_tensor_tensor(
+                    out=nb[:, t : t + 1],
+                    in0=mx[:, t, NCH - 1 : NCH],
+                    scalar=mu[:, t : t + 1],
+                    in1=nrcn[:, t : t + 1],
+                    op0=ALU.max,
+                    op1=ALU.mult,
+                )
 
             units = [[0], [1]] + [[2 * k, 2 * k + 1] for k in range(1, NBLK)]
             es = {}

@@ -23,9 +23,9 @@ NB = 3
 DEF = 12
 SEV = [2, 2]
 AHEAD = 3
-FILLB = [3, 3, 3, 3, 3, 2, 2, 2]
+FILLB = [3, 3, 3, 3, 3, 3, 3, 3]
 SCHED = [("T", 0), ("gram", 1), ("ev2a", 3), ("recip", 2), ("ev2b", 3), ("ev1", 2), ("back", 2), ("evTs", 0), ("rg", 0), ("q1", 1), ("mm1", 1), ("gx", 1), ("q2", 0), ("evT", 0), ("rgg", -1), ("load", -3), ("norms", -1), ("roots", 1), ("norms2", -1), ("floor", 1)]
-RUNOUT = [("gram", 1), ("gx", 1), ("roots", 1), ("q1", 1), ("mm1", 1), ("recip", 2), ("ev1", 2), ("floor", 1), ("back", 2), ("ev2", 3), ("load", -3)]
+RUNOUT = [("gram", 1), ("gx", 1), ("roots", 1), ("floor", 1), ("q1", 1), ("mm1", 1), ("recip", 2), ("recipl", 1), ("ev1", 2), ("back", 2), ("ev2", 3), ("load", -3)]
 
 
 def tile_ca3_recurrentmatrix_pa_kernel(tc, current, memory_matrix, out):
@@ -261,7 +261,15 @@ def tile_ca3_recurrentmatrix_pa_kernel(tc, current, memory_matrix, out):
                     out=nrmc[:, 4 * i : 4 * i + 4], in_=nrm[:, 4 * i : 4 * i + 4, :], axis=AX.X, op=ALU.max
                 )
 
+            def recip_last(i):
+                if i == NCH - 1:
+                    recip_now(i)
+
             def recip(i):
+                if i < NCH - 1:
+                    recip_now(i)
+
+            def recip_now(i):
                 nc.vector.reciprocal(out=rmn[:, 4 * i : 4 * i + 4], in_=nrmc[:, 4 * i : 4 * i + 4])
 
             def quant1(i):
@@ -361,7 +369,7 @@ def tile_ca3_recurrentmatrix_pa_kernel(tc, current, memory_matrix, out):
                 nc.vector.quantize_mx(out=ccodes[:].bitcast(FP8X4), scales=cscales[:], in_=gcur[:])
 
             ops = {
-                "T": transposes, "evT": ev_v, "evTs": ev_s, "norms": norms, "recip": recip, "floor": floor, "gram": gram, "gx": gram_diag, "roots": roots, "norms2": norms_last, "q1": quant1, "mm1": mm1,
+                "T": transposes, "evT": ev_v, "evTs": ev_s, "norms": norms, "recip": recip, "recipl": recip_last, "floor": floor, "gram": gram, "gx": gram_diag, "roots": roots, "norms2": norms_last, "q1": quant1, "mm1": mm1,
                 "ev1": evac1, "back": back, "ev2": evac2, "ev2a": evac2_first, "ev2b": evac2_second, "rg": rg, "q2": q2, "rgg": rgg,
             }
 
@@ -379,6 +387,9 @@ def tile_ca3_recurrentmatrix_pa_kernel(tc, current, memory_matrix, out):
             for i in range(-nlag):
                 norms(i)
                 norms_last(i)
+            for t in range(2):
+                nc.scalar.activation(out=junk[t], in_=curt[:, t, :], func=ACT.Square, accum_out=cn2[:, t : t + 1])
+            nc.scalar.sqrt(out=cnrm[:], in_=cn2[:])
             whole(0)
             vcopy(g2w[0][:], nat[0][:])
             nc.vector.quantize_mx(
@@ -388,13 +399,6 @@ def tile_ca3_recurrentmatrix_pa_kernel(tc, current, memory_matrix, out):
             q2done.add((0, 1))
             last = max(lag for (op, lag) in SCHED)
             for i in range(NCH + last + 1):
-                if i == NCH:
-                    junkc = pha.tile([P, 2, D], BF16, name="junkc", tag="g1", bufs=2, align_bytes=64)
-                    for t in range(2):
-                        nc.scalar.activation(
-                            out=junkc[:, t, :], in_=curt2[:, t, :], func=ACT.Square, accum_out=cn2[:, t : t + 1]
-                        )
-                    nc.scalar.sqrt(out=cnrm[:], in_=cn2[:])
                 for op, lag in SCHED if i < NCH else RUNOUT:
                     c = i - lag
                     if op == "load":
@@ -411,12 +415,13 @@ def tile_ca3_recurrentmatrix_pa_kernel(tc, current, memory_matrix, out):
                     nc.scalar.activation(out=one2[:], in_=one[:], func=ACT.Exp)
                 if i == NCH + 1:
                     nc.scalar.activation(out=cur02[:], in_=curt2[:], func=ACT.Copy, scale=0.2)
-                if i == NCH:
+                if i == 1:
                     nc.vector.tensor_scalar_max(out=cnrmc[:], in0=cnrm[:], scalar1=EPS)
-                if i == NCH:
+                if i == 2:
                     nc.vector.reciprocal(out=rcn[:], in_=cnrmc[:])
-                if i == NCH + 1:
+                if i == 3:
                     nc.vector.tensor_scalar_mul(out=nrcn[:], in0=rcn[:], scalar1=-1.0)
+                if i == NCH + 1:
                     nc.vector.tensor_reduce(out=mu[:], in_=mx[:, :, : NCH - 1], axis=AX.X, op=ALU.max)
                 if i == d0:
                     nc.sync.dma_start(out=curt2[:], in_=current.rearrange("(t p) d -> p t d", p=P))
@@ -523,13 +528,14 @@ def tile_ca3_recurrentmatrix_pa_kernel(tc, current, memory_matrix, out):
                     quante(x + 1)
                     if x + 3 < len(units):
                         exps(x + 3)
-                    if x + 2 == len(units):
+                    if x + 3 == len(units):
                         nc.vector.tensor_reduce(out=rsum[:], in_=rs[:], axis=AX.X, op=ALU.add)
                         some_left(1)
                         nc.vector.reciprocal(out=rinv[:], in_=rsum[:])
                         some_left(1)
                         nc.vector.tensor_scalar_mul(out=wgt[:], in0=rinv[:], scalar1=0.8)
-                    some_left(FILLB[x])
+                    else:
+                        some_left(FILLB[x])
             for h in range(2):
                 for t in range(2):
                     o = phb.tile([P, 512], F32, name="o", tag="o", bufs=4)

from contextlib import ExitStack

import concourse.mybir as mybir
from concourse.masks import make_identity

F32 = mybir.dt.float32
BF16 = mybir.dt.bfloat16
U32 = mybir.dt.uint32
U8 = mybir.dt.uint8
FP8X4 = mybir.dt.float8_e4m3fn_x4
ALU = mybir.AluOpType
ACT = mybir.ActivationFunctionType
AX = mybir.AxisListType

B, C, D = 256, 8192, 1024
FLOPS = 2 * 2 * B * C * D
EPS = 1e-8
P = 128
CH = 512
NCH = C // CH
NBLK = NCH // 2
NB = 3
DEF = 12
SEV = [2, 2]
AHEAD = 3
FILLB = [3, 3, 3, 3, 3, 3, 3, 3]
SCHED = [("T", 0), ("gram", 1), ("ev2a", 3), ("recip", 2), ("ev2b", 3), ("ev1", 2), ("back", 2), ("evTs", 0), ("rg", 0), ("q1", 1), ("mm1", 1), ("gx", 1), ("q2", 0), ("evT", 0), ("rgg", -1), ("load", -3), ("norms", -1), ("roots", 1), ("norms2", -1), ("floor", 1)]
RUNOUT = [("gram", 1), ("gx", 1), ("roots", 1), ("floor", 1), ("q1", 1), ("mm1", 1), ("recip", 2), ("recipl", 1), ("ev1", 2), ("back", 2), ("ev2", 3), ("load", -3)]


def tile_ca3_recurrentmatrix_pa_kernel(tc, current, memory_matrix, out):
    nc = tc.nc
    with ExitStack() as ctx:
        ctx.enter_context(tc.manual_schedule())
        keep = ctx.enter_context(tc.tile_pool(name="keep", bufs=1))
        both = ctx.enter_context(tc.tile_pool(name="both", bufs=2))
        psT = ctx.enter_context(tc.psum_pool(name="psT", bufs=4))
        psD = ctx.enter_context(tc.psum_pool(name="psD", bufs=2))
        psU = ctx.enter_context(tc.psum_pool(name="psU", bufs=2))

        ident_f = keep.tile([P, P], F32, name="ident_f")
        codes2 = keep.tile([P, NCH, D], U32, name="codes2", align_bytes=64)
        scales2 = keep.tile([P, NCH, D], U8, name="scales2", align_bytes=64)
        sim = keep.tile([P, 2, C], F32, name="sim")
        cur02 = keep.tile([P, 2, D], F32, name="cur02")
        curt2 = keep.tile([P, 2, D], BF16, name="curt2")
        ccodes = keep.tile([P, 512], U32, name="ccodes", align_bytes=64)
        cscales = keep.tile([P, 512], U8, name="cscales", align_bytes=64)
        n2 = keep.tile([P, 4 * NCH], F32, name="n2")
        nrm = keep.tile([P, 4 * NCH, 2], F32, name="nrm")
        nrmc = keep.tile([P, 4 * NCH], F32, name="nrmc")
        rmn = keep.tile([P, 4 * NCH], F32, name="rmn")
        cn2 = keep.tile([P, 2], F32, name="cn2")
        cnrm = keep.tile([P, 2], F32, name="cnrm")
        cnrmc = keep.tile([P, 2], F32, name="cnrmc")
        rcn = keep.tile([P, 2], F32, name="rcn")
        nrcn = keep.tile([P, 2], F32, name="nrcn")
        mx = keep.tile([P, 2, NCH], F32, name="mx")
        mu = keep.tile([P, 2], F32, name="mu")
        nb = keep.tile([P, 2], F32, name="nb")
        rs = keep.tile([P, 2, NBLK + 1], F32, name="rs")
        rsum = keep.tile([P, 2], F32, name="rsum")
        rinv = keep.tile([P, 2], F32, name="rinv")
        wgt = keep.tile([P, 2], F32, name="wgt")
        one = keep.tile([P, 1], F32, name="one")
        one2 = keep.tile([P, 1], F32, name="one2")

        nat = {}
        g2w = {}
        g2h = {}
        d0 = NCH - DEF
        q2done = set()

        def load(i, first=False):
            if i < NCH + DEF:
                if i >= NCH:
                    i = i - DEF
                t = both.tile([P, 4, D], BF16, name="nat", tag="nat", bufs=NB)
                src = memory_matrix[i * CH : (i + 1) * CH, :].rearrange("(p j) d -> p j d", j=4)
                if first:
                    for j in range(4):
                        nc.sync.dma_start(out=t[:, j : j + 1, :], in_=src[:, j : j + 1, :])
                else:
                    nc.sync.dma_start(out=t[:], in_=src)
                nat[i] = t

        def vcopy(dst, src):
            nc.vector.tensor_copy(
                out=dst.rearrange("p (c i) t -> p c t i", i=4), in_=src.rearrange("p t (c i) -> p c t i", i=4)
            )

        def whole(i):
            g2w[i] = both.tile([P, D, 4], BF16, name="g2w", tag="g2w", bufs=1, align_bytes=64)

        def rgg(i):
            whole(i)
            nc.gpsimd.tensor_scalar(
                out=g2w[i][:, :512, :],
                in0=nat[i][:, :, :512].rearrange("p t w -> p w t"),
                scalar1=1.0,
                scalar2=0.0,
                op0=ALU.mult,
                op1=ALU.add,
            )

        def rg(i):
            if 0 < i < d0:
                vcopy(g2w[i][:, 512:, :], nat[i][:, :, 512:])

        def q2(i):
            if i == 0:
                return
            w = D if i < d0 else 512
            nc.vector.quantize_mx(
                out=codes2[:, i, :w].bitcast(FP8X4),
                scales=scales2[:, i, :w],
                in_=g2w[i][:, :w, :].rearrange("p w t -> p (w t)"),
            )
            q2done.add((i, 0))
            if i < d0:
                q2done.add((i, 1))

        def regroup_half(i, eng):
            t = both.tile([P, 512, 4], BF16, name="g2h", tag="g2h", bufs=3, align_bytes=64)
            if eng == "v":
                vcopy(t[:], nat[i][:, :, 512:])
            elif eng == "g":
                nc.gpsimd.tensor_scalar(
                    out=t[:],
                    in0=nat[i][:, :, 512:].rearrange("p t w -> p w t"),
                    scalar1=1.0,
                    scalar2=0.0,
                    op0=ALU.mult,
                    op1=ALU.add,
                )
            else:
                nc.scalar.copy(out=t[:], in_=nat[i][:, :, 512:].rearrange("p t w -> p w t"))
            g2h[i] = t

        def quant_half(i):
            q2done.add((i, 1))
            nc.vector.quantize_mx(
                out=codes2[:, i, 512:].bitcast(FP8X4),
                scales=scales2[:, i, 512:],
                in_=g2h[i][:].rearrange("p w t -> p (w t)"),
            )

        late = list(range(d0, NCH))
        left = [("r", i) for i in late[:AHEAD]]
        for n, i in enumerate(late):
            left += [("q", i)]
            if n + AHEAD < len(late):
                left += [("r", late[n + AHEAD])]
        done = [0]

        def late_engine(n):
            return "v"

        def some_left(n):
            for x in range(n):
                if done[0] < len(left):
                    kind, i = left[done[0]]
                    done[0] += 1
                    if kind == "r":
                        regroup_half(i, late_engine(i - d0))
                    else:
                        quant_half(i)

        with tc.tile_pool(name="pha", bufs=2) as pha:
            g1 = {}
            bG = {}
            junkv = pha.tile([P, P], F32, name="junkv", bufs=1)
            c1 = {}
            bT = {}
            bD = {}
            bU = {}
            uTs = {}
            junk = [sim[:, n % 2, (NCH - 1 - n // 2) * CH : (NCH - n // 2) * CH].bitcast(BF16) for n in range(4)]

            def transposes(i):
                nat32 = nat[i][:].bitcast(F32)
                for b in range(4):
                    G, k = b // 2, b % 2
                    bank = psT.tile([P, 512], F32, name="bankT", tag="T")
                    for jj in range(2):
                        for u in range(2):
                            nc.tensor.transpose(
                                bank[:, (jj * 2 + u) * 128 : (jj * 2 + u + 1) * 128],
                                nat32[:, 2 * k + jj, G * 256 + u * 128 : G * 256 + (u + 1) * 128],
                                ident_f[:],
                            )
                    bT[(i, b)] = bank

            def vshare(i):
                return 4 if i == 0 else 0 if i < d0 else 1

            def evac_t(i, eng):
                if i not in g1:
                    g1[i] = pha.tile([P, 4096], BF16, name="g1", tag="g1", bufs=2, align_bytes=64)
                g32 = g1[i][:].bitcast(F32)
                for b in range(4):
                    on_v = b >= 4 - vshare(i)
                    if on_v != (eng == "v"):
                        continue
                    dst = g32[:, b * 512 : (b + 1) * 512].rearrange("p (j c u) -> p j c u", j=2, u=2)
                    src = bT[(i, b)][:].rearrange("p (j u c) -> p j c u", j=2, u=2)
                    if on_v:
                        nc.vector.tensor_copy(out=dst, in_=src)
                    else:
                        nc.scalar.copy(out=dst, in_=src)

            def ev_v(i):
                evac_t(i, "v")

            def ev_s(i):
                evac_t(i, "s")

            def ngram(i):
                return 1 if i < 15 else 0

            def gram(i):
                if ngram(i) == 0:
                    return
                bank = psT.tile([P, 512], F32, name="bankG", tag="T")
                for n in range(ngram(i)):
                    k, jj = (3 - n) // 2, (3 - n) % 2
                    for x in range(8):
                        lo = ((x // 4 * 2 + k) * 2 + jj) * 512
                        a = g1[i][:, lo + x % 4 : lo + 512 : 4]
                        nc.tensor.matmul(bank[:, n * 128 : (n + 1) * 128], a, a, start=(x == 0), stop=(x == 7))
                bG[i] = bank

            def gram_diag(i):
                for n in range(ngram(i)):
                    j = 3 - n
                    nc.vector.scalar_tensor_tensor(
                        out=junkv[:],
                        in0=bG[i][:, n * 128 : (n + 1) * 128],
                        scalar=1.0,
                        in1=ident_f[:],
                        op0=ALU.mult,
                        op1=ALU.mult,
                        accum_out=n2[:, 4 * i + j : 4 * i + j + 1],
                    )

            def norms_last(i):
                norms(i, True)

            def norms(i, last=False):
                m = 4 - ngram(i)
                for j in range(m - 1, m) if last else range(m - 1):
                    nc.scalar.activation(
                        out=junk[j], in_=nat[i][:, j, :], func=ACT.Square, accum_out=n2[:, 4 * i + j : 4 * i + j + 1]
                    )

            def roots(i):
                nc.scalar.sqrt(out=nrm[:, 4 * i : 4 * i + 4, 0], in_=n2[:, 4 * i : 4 * i + 4])

            def floor(i):
                nc.vector.tensor_reduce(
                    out=nrmc[:, 4 * i : 4 * i + 4], in_=nrm[:, 4 * i : 4 * i + 4, :], axis=AX.X, op=ALU.max
                )

            def recip_last(i):
                if i == NCH - 1:
                    recip_now(i)

            def recip(i):
                if i < NCH - 1:
                    recip_now(i)

            def recip_now(i):
                nc.vector.reciprocal(out=rmn[:, 4 * i : 4 * i + 4], in_=nrmc[:, 4 * i : 4 * i + 4])

            def quant1(i):
                c = pha.tile([P, 1024], U32, name="c1", tag="c1", bufs=1, align_bytes=64)
                s = pha.tile([P, 1024], U8, name="s1", tag="s1", bufs=1, align_bytes=64)
                nc.vector.quantize_mx(out=c[:].bitcast(FP8X4), scales=s[:], in_=g1[i][:])
                c1[i] = (c, s)

            def mm1(i):
                c, s = c1[i]
                for k in range(2):
                    if i == NCH - 1:
                        bank = psT.tile([P, 512], F32, name="bankD2", tag="T")
                    else:
                        bank = psD.tile([P, 512], F32, name="bankD", tag="D")
                    for jj in range(2):
                        for G in range(2):
                            lo = G * 512 + (2 * k + jj) * 128
                            nc.tensor.matmul_mx(
                                out=bank[:, jj * 256 : (jj + 1) * 256],
                                lhsT=c[:, lo : lo + 128].bitcast(FP8X4),
                                lhsT_scale=s[:, lo : lo + 128],
                                rhs=ccodes[:, G * 256 : (G + 1) * 256].bitcast(FP8X4),
                                rhs_scale=cscales[:, G * 256 : (G + 1) * 256],
                                start=(G == 0),
                                stop=(G == 1),
                            )
                    bD[(i, k)] = bank

            def evac1(i):
                uT = pha.tile([P, 4, 256], F32, name="uT", tag="uT", bufs=2)
                for k in range(2):
                    if i >= NCH - 1:
                        for j in range(2 * k, 2 * k + 2):
                            nc.scalar.activation(
                                out=uT[:, j, :],
                                in_=bD[(i, k)][:, (j % 2) * 256 : (j % 2 + 1) * 256],
                                func=ACT.Copy,
                                scale=rmn[:, 4 * i + j : 4 * i + j + 1],
                            )
                        continue
                    nc.vector.tensor_tensor(
                        out=uT[:, 2 * k : 2 * k + 2, :],
                        in0=bD[(i, k)][:].rearrange("p (j b) -> p j b", j=2),
                        in1=rmn[:, 4 * i + 2 * k : 4 * i + 2 * k + 2].unsqueeze(2).to_broadcast([P, 2, 256]),
                        op=ALU.mult,
                    )
                uTs[i] = uT

            def back(i):
                for t in range(2):
                    if i == NCH - 1:
                        bank = psT.tile([P, 512], F32, name="bankU2", tag="T")
                    else:
                        bank = psU.tile([P, 512], F32, name="bankU", tag="U")
                    for j in range(4):
                        nc.tensor.transpose(
                            bank[:, j * 128 : (j + 1) * 128], uTs[i][:, j, t * 128 : (t + 1) * 128], ident_f[:]
                        )
                    bU[(i, t)] = bank

            def evac2_first(i):
                evac2(i, (0,))

            def evac2_second(i):
                evac2(i, (1,))

            def evac2(i, halves=(0, 1)):
                for t in halves:
                    nc.vector.tensor_scalar(
                        out=sim[:, t, i * CH : (i + 1) * CH].rearrange("p (u n e) -> p u n e", u=2, e=2),
                        in0=bU[(i, t)][:].rearrange("p (u e n) -> p u n e", u=2, e=2),
                        scalar1=1.0,
                        scalar2=None,
                        op0=ALU.mult,
                        op1=ALU.max,
                        accum_out=mx[:, t, i : i + 1],
                    )

            def cur_path():
                cur32 = curt[:].bitcast(F32)
                gcur = pha.tile([P, 2048], BF16, name="gcur", tag="c1", bufs=1, align_bytes=64)
                gcur32 = gcur[:].bitcast(F32)
                for G in range(2):
                    bank = psT.tile([P, 512], F32, name="bankT", tag="T")
                    for u in range(2):
                        for t in range(2):
                            nc.tensor.transpose(
                                bank[:, u * 256 + t * 128 : u * 256 + (t + 1) * 128],
                                cur32[:, t, G * 256 + u * 128 : G * 256 + (u + 1) * 128],
                                ident_f[:],
                            )
                    nc.vector.tensor_copy(
                        out=gcur32[:, G * 512 : (G + 1) * 512].rearrange("p (b u) -> p b u", u=2),
                        in_=bank[:].rearrange("p (u b) -> p b u", u=2),
                    )
                nc.vector.quantize_mx(out=ccodes[:].bitcast(FP8X4), scales=cscales[:], in_=gcur[:])

            ops = {
                "T": transposes, "evT": ev_v, "evTs": ev_s, "norms": norms, "recip": recip, "recipl": recip_last, "floor": floor, "gram": gram, "gx": gram_diag, "roots": roots, "norms2": norms_last, "q1": quant1, "mm1": mm1,
                "ev1": evac1, "back": back, "ev2": evac2, "ev2a": evac2_first, "ev2b": evac2_second, "rg": rg, "q2": q2, "rgg": rgg,
            }

            nc.vector.memset(one[:], 1.0)
            nc.vector.memset(nrm[:], EPS)
            nc.scalar.sqrt(out=one2[:], in_=one[:])
            make_identity(nc, ident_f[:])
            load(0, True)
            curt = pha.tile([P, 2, D], BF16, name="curt", tag="uT", bufs=2)
            nc.sync.dma_start(out=curt[:], in_=current.rearrange("(t p) d -> p t d", p=P))
            for i in range(1, NB):
                load(i)

            nlag = [lag for (op, lag) in SCHED if op == "norms"][0]
            for i in range(-nlag):
                norms(i)
                norms_last(i)
            for t in range(2):
                nc.scalar.activation(out=junk[t], in_=curt[:, t, :], func=ACT.Square, accum_out=cn2[:, t : t + 1])
            nc.scalar.sqrt(out=cnrm[:], in_=cn2[:])
            whole(0)
            vcopy(g2w[0][:], nat[0][:])
            nc.vector.quantize_mx(
                out=codes2[:, 0, :].bitcast(FP8X4), scales=scales2[:, 0, :], in_=g2w[0][:].rearrange("p w t -> p (w t)")
            )
            q2done.add((0, 0))
            q2done.add((0, 1))
            last = max(lag for (op, lag) in SCHED)
            for i in range(NCH + last + 1):
                for op, lag in SCHED if i < NCH else RUNOUT:
                    c = i - lag
                    if op == "load":
                        if NB <= c:
                            load(c)
                    elif op in ("norms", "norms2"):
                        if -lag <= c < NCH:
                            ops[op](c)
                    elif 0 <= c < NCH and (c > 0 or lag >= 0):
                        ops[op](c)
                if i == 0:
                    cur_path()
                if i == NCH:
                    nc.scalar.activation(out=one2[:], in_=one[:], func=ACT.Exp)
                if i == NCH + 1:
                    nc.scalar.activation(out=cur02[:], in_=curt2[:], func=ACT.Copy, scale=0.2)
                if i == 1:
                    nc.vector.tensor_scalar_max(out=cnrmc[:], in0=cnrm[:], scalar1=EPS)
                if i == 2:
                    nc.vector.reciprocal(out=rcn[:], in_=cnrmc[:])
                if i == 3:
                    nc.vector.tensor_scalar_mul(out=nrcn[:], in0=rcn[:], scalar1=-1.0)
                if i == NCH + 1:
                    nc.vector.tensor_reduce(out=mu[:], in_=mx[:, :, : NCH - 1], axis=AX.X, op=ALU.max)
                if i == d0:
                    nc.sync.dma_start(out=curt2[:], in_=current.rearrange("(t p) d -> p t d", p=P))
            for c in range(NCH + last + 1 + NB, NCH + DEF):
                load(c)

        with tc.tile_pool(name="phb", bufs=2) as phb:
            for t in range(2):
                nc.vector.scalar_tensor_tensor(
                    out=nb[:, t : t + 1],
                    in0=mx[:, t, NCH - 1 : NCH],
                    scalar=mu[:, t : t + 1],
                    in1=nrcn[:, t : t + 1],
                    op0=ALU.max,
                    op1=ALU.mult,
                )

            units = [[0], [1]] + [[2 * k, 2 * k + 1] for k in range(1, NBLK)]
            es = {}
            bE = {}
            ges = {}
            ecs = {}
            acc = [
                [psD.tile([P, 512], F32, name="acc%d" % h, tag="D") for h in range(2)],
                [psU.tile([P, 512], F32, name="acc%d" % (2 + h), tag="U") for h in range(2)],
            ]

            def exps(x):
                g0, n = units[x][0], len(units[x])
                for t in range(2):
                    e = phb.tile([P, 2 * CH], BF16, name="e", tag="e", bufs=6)
                    nc.scalar.activation(
                        out=e[:, : n * CH],
                        in_=sim[:, t, g0 * CH : (g0 + n) * CH],
                        func=ACT.Exp,
                        bias=nb[:, t : t + 1],
                        scale=rcn[:, t : t + 1],
                        accum_out=rs[:, t, x : x + 1],
                    )
                    es[(x, t)] = e

            def etrans(x):
                for gg in range(len(units[x])):
                    bank = psT.tile([P, 512], F32, name="bankE", tag="T")
                    for t in range(2):
                        words = es[(x, t)][:].bitcast(F32)
                        for u in range(2):
                            nc.tensor.transpose(
                                bank[:, u * 256 + t * 128 : u * 256 + (t + 1) * 128],
                                words[:, gg * 256 + u * 128 : gg * 256 + (u + 1) * 128],
                                ident_f[:],
                            )
                    bE[(x, gg)] = bank

            def evac3(x):
                ge = phb.tile([P, 2048], BF16, name="ge", tag="ge", bufs=2, align_bytes=64)
                for gg in range(len(units[x])):
                    dst = ge[:].bitcast(F32)[:, gg * 512 : (gg + 1) * 512].rearrange("p (b u) -> p b u", u=2)
                    src = bE[(x, gg)][:].rearrange("p (u b) -> p b u", u=2)
                    if x >= SEV[gg]:
                        nc.scalar.copy(out=dst, in_=src)
                    else:
                        nc.vector.tensor_copy(out=dst, in_=src)
                ges[x] = ge

            def quante(x):
                w = 256 * len(units[x])
                cd = phb.tile([P, 512], U32, name="ec", tag="ec", bufs=2, align_bytes=64)
                s = phb.tile([P, 512], U8, name="esc", tag="esc", bufs=2, align_bytes=64)
                nc.vector.quantize_mx(out=cd[:, :w].bitcast(FP8X4), scales=s[:, :w], in_=ges[x][:, : 4 * w])
                ecs[x] = (cd, s)

            def mm2(x, h):
                cd, s = ecs[x]
                for t in range(2):
                    for gg, g in enumerate(units[x]):
                        lo = gg * 256 + t * 128
                        nc.tensor.matmul_mx(
                            out=acc[t][h][:],
                            lhsT=cd[:, lo : lo + 128].bitcast(FP8X4),
                            lhsT_scale=s[:, lo : lo + 128],
                            rhs=codes2[:, g, h * 512 : (h + 1) * 512].bitcast(FP8X4),
                            rhs_scale=scales2[:, g, h * 512 : (h + 1) * 512],
                            start=(g == 0),
                            stop=(g == NCH - 1),
                        )

            exps(0)
            exps(1)
            exps(2)
            etrans(0)
            some_left(2)
            evac3(0)
            quante(0)
            for x in range(len(units)):
                if x + 1 < len(units):
                    etrans(x + 1)
                for h in range(2):
                    while any((g, h) not in q2done for g in units[x]):
                        some_left(1)
                    mm2(x, h)
                if x + 1 < len(units):
                    evac3(x + 1)
                    quante(x + 1)
                    if x + 3 < len(units):
                        exps(x + 3)
                    if x + 3 == len(units):
                        nc.vector.tensor_reduce(out=rsum[:], in_=rs[:], axis=AX.X, op=ALU.add)
                        some_left(1)
                        nc.vector.reciprocal(out=rinv[:], in_=rsum[:])
                        some_left(1)
                        nc.vector.tensor_scalar_mul(out=wgt[:], in0=rinv[:], scalar1=0.8)
                    else:
                        some_left(FILLB[x])
            for h in range(2):
                for t in range(2):
                    o = phb.tile([P, 512], F32, name="o", tag="o", bufs=4)
                    nc.vector.scalar_tensor_tensor(
                        out=o[:],
                        in0=acc[t][h][:],
                        scalar=wgt[:, t : t + 1],
                        in1=cur02[:, t, h * 512 : (h + 1) * 512],
                        op0=ALU.mult,
                        op1=ALU.add,
                    )
                    nc.sync.dma_start(out=out[t * P : (t + 1) * P, h * 512 : (h + 1) * 512], in_=o[:])
